import numpy as np
import ml_dtypes


def mxq(x, axis, fmt="e4m3"):
    dtype, down = {"e4m3": (ml_dtypes.float8_e4m3fn, 7), "e5m2": (ml_dtypes.float8_e5m2, 14)}[fmt]
    v = np.moveaxis(np.asarray(x, np.float32).astype(ml_dtypes.bfloat16).astype(np.float64), axis, -1)
    blocks = v.reshape(v.shape[:-1] + (-1, 32))
    amax = np.abs(blocks).max(-1, keepdims=True)
    byte = np.maximum(np.where(amax > 0, np.frexp(amax)[1] - 1 + 127, 0) - down, 1)
    scale = np.exp2(byte - 127.0)
    codes = (blocks / scale).astype(np.float32).astype(dtype).astype(np.float64)
    return np.moveaxis((codes * scale).reshape(v.shape), -1, axis)


WIDE = False


def mx_kscale(k):
    if not WIDE:
        return np.ones(k)
    levels = np.array([30, -30])
    if k % 512:
        return np.exp2(np.random.permutation(np.resize(levels, k // 32))).repeat(32)
    a = np.empty((k // 512, 16))
    for p in range(k // 512):
        a[p, :8] = np.random.permutation(np.resize(levels, 8))
        for g in range(8):
            far = levels[np.abs(levels - a[p, g]) >= 10]
            a[p, g + 8] = far[np.random.randint(len(far))]
    return np.exp2(a.ravel()).repeat(32)


BF16 = ml_dtypes.bfloat16


def bf(x):
    return np.asarray(x, np.float32).astype(BF16)


def f64(x):
    return np.asarray(x).astype(np.float64)


B, IN, OUT = 512, 2048, 2048


def setup_inputs():
    s = mx_kscale(IN)
    return {"input_data": bf(np.random.standard_normal((B, IN)) * s),
            "weight": bf(np.random.standard_normal((OUT, IN)) / np.sqrt(IN) / s),
            "bias": bf(np.random.standard_normal(OUT) * 0.5),
            "prev_grad": bf(np.random.standard_normal((OUT, IN)) / np.sqrt(IN) / s),
            "prev_bias_grad": bf(np.random.standard_normal(OUT) * 0.5),
            "lr_samples": bf(np.random.uniform(0.1, 1.0, B))}


def reference(input_data, weight, bias, prev_grad, prev_bias_grad, lr_samples):
    xq = mxq(f64(input_data), 1, "e5m2")
    base = (xq @ mxq(f64(weight), 1, "e4m3").T) + f64(bias)
    pert = (xq @ mxq(f64(prev_grad), 1, "e4m3").T) + f64(prev_bias_grad)
    return base - f64(lr_samples)[:, None] * pert

@@ -1,0 +1,217 @@
+from contextlib import ExitStack
+
+import concourse.mybir as mybir
+from concourse.masks import make_identity
+
+B, IN, OUT = 512, 2048, 2048
+FLOPS = 2 * 2 * B * IN * OUT
+
+F32 = mybir.dt.float32
+BF16 = mybir.dt.bfloat16
+U32 = mybir.dt.uint32
+U8 = mybir.dt.uint8
+E4 = mybir.dt.float8_e4m3fn_x4
+E5 = mybir.dt.float8_e5m2_x4
+ALU = mybir.AluOpType
+
+P = 128
+NT = 4
+NJ = 4
+NG = 4
+NUNIT = 36
+NSTEP = NUNIT // 2
+RAW_BUFS = 8
+
+LEAD = 2
+HEADN = 6
+
+
+def tile_optimizedlinear_kernel(tc, input_data, weight, bias, prev_grad, prev_bias_grad, lr_samples, out):
+    nc = tc.nc
+    SHUF = {q: (None if q < 8 else "V" if q % 4 != 3 else "S") for q in range(NUNIT)}
+    EVAC = {(s, i): ("V" if (s < 4 and i % 2 == 1) else "S") for s in range(NSTEP) for i in range(4)}
+    DSTEP = {i: i for i in range(16)}
+    DEVAC = {i: "S" for i in range(16)}
+    x_v = input_data.rearrange("(p t) k -> p t k", t=NT)
+    out_v = out.rearrange("(p t) o -> p t o", t=NT)
+
+    with ExitStack() as ctx:
+        const = ctx.enter_context(tc.tile_pool(name="const", bufs=1))
+        rawp = ctx.enter_context(tc.tile_pool(name="rawp", bufs=1))
+        work = ctx.enter_context(tc.tile_pool(name="work", bufs=1))
+        tps = ctx.enter_context(tc.psum_pool(name="tps", bufs=4))
+        acp = ctx.enter_context(tc.psum_pool(name="acp", bufs=4))
+
+        def cp(who, dst, src):
+            if who == "V":
+                nc.vector.tensor_copy(out=dst, in_=src)
+            else:
+                nc.scalar.copy(out=dst, in_=src)
+
+        ident = const.tile([P, P], F32, name="ident")
+        make_identity(nc, ident[:])
+        rrows = const.tile([P, OUT], BF16, name="rrows")
+        lrows = const.tile([P, B], BF16, name="lrows")
+        lperm = const.tile([P, NT, P], BF16, name="lperm")
+        lr_pt = const.tile([P, NT], BF16, name="lr_pt")
+        nlr = const.tile([P, NT], F32, name="nlr")
+        nc.vector.memset(lrows[:], 0.0)
+        nc.vector.memset(lrows[0:1, :], -1.0)
+        nc.vector.memset(rrows[:], 0.0)
+        nc.scalar.dma_start(out=lrows[1:2, :], in_=lr_samples.rearrange("(o n) -> o n", o=1))
+        nc.scalar.dma_start(out=rrows[0:1, :], in_=bias.rearrange("(o n) -> o n", o=1))
+        nc.scalar.dma_start(out=rrows[1:2, :], in_=prev_bias_grad.rearrange("(o n) -> o n", o=1))
+        nc.scalar.dma_start(out=lr_pt[:], in_=lr_samples.rearrange("(p t) -> p t", t=NT))
+
+        raw = {}
+
+        def load(d):
+            if d < NT:
+                r = rawp.tile([P, IN], BF16, name="xr%d" % d, tag="xr", bufs=NT, align_bytes=64)
+                nc.sync.dma_start(out=r[:], in_=x_v[:, d, :])
+            else:
+                i = d - NT
+                mat = weight if (i // 2) % 2 == 0 else prev_grad
+                j, h = i // 4, i % 2
+                r = rawp.tile([P, 4, IN // 2], BF16, name="wr%d" % i, tag="wr", bufs=RAW_BUFS, align_bytes=64)
+                nc.sync.dma_start(
+                    out=r[:],
+                    in_=mat[512 * j : 512 * (j + 1), 1024 * h : 1024 * (h + 1)].rearrange("(a r) k -> r a k", a=4),
+                )
+            raw[d] = r
+
+        NLOAD = NT + 16
+        for d in range(NT + RAW_BUFS):
+            load(d)
+
+        nc.vector.tensor_copy(out=lperm[:], in_=lrows[:].rearrange("p (m t) -> p t m", t=NT))
+        nc.vector.tensor_scalar(out=nlr[:], in0=lr_pt[:], scalar1=-1.0, scalar2=None, op0=ALU.mult)
+
+        def unit_words(q):
+            if q < NT:
+                return raw[q][:].bitcast(F32).rearrange("p (a w u) -> p a u w", a=4, u=2)
+            i, gl = (q - NT) // 2, q % 2
+            return raw[NT + i][:].bitcast(F32)[:, :, 256 * gl : 256 * (gl + 1)].rearrange("p a (w u) -> p a u w", u=2)
+
+        src = {}
+        banks = {}
+        grp = {}
+        codes = {}
+        scl = {}
+        dtile = {}
+        accs = {}
+
+        def shuffle(q):
+            if SHUF[q] is None:
+                src[q] = unit_words(q)
+                return
+            s = work.tile([P, 4, 2, P], F32, name="sh%d" % q, tag="sh", bufs=2 * LEAD + 2, align_bytes=64)
+            cp(SHUF[q], s[:], unit_words(q))
+            src[q] = s[:]
+
+        def transposes(q):
+            for h in range(2):
+                bk = tps.tile([P, 4, P], F32, name="tb%d_%d" % (q, h), tag="tb", bufs=4)
+                banks[(q, h)] = bk
+                for i in range(4):
+                    nc.tensor.transpose(out=bk[:, i, :], in_=src[q][:, 2 * h + i // 2, i % 2, :], identity=ident[:])
+
+        def evacuate(q, h, who):
+            if h == 0:
+                grp[q] = work.tile([P, 4 * 512], BF16, name="gr%d" % q, tag="gr", bufs=4, align_bytes=64)
+            dst = grp[q][:].bitcast(F32).rearrange("p (a r u) -> p a r u", a=4, u=2)[:, 2 * h : 2 * h + 2, :, :]
+            cp(who, dst, banks[(q, h)][:].rearrange("p (a u) r -> p a r u", u=2))
+
+        def quantize(q):
+            if q < NT:
+                c = work.tile([P, 512], U32, name="xc%d" % q, tag="xc", bufs=NT, align_bytes=64)
+                s = work.tile([P, 512], U8, name="xs%d" % q, tag="xs", bufs=NT, align_bytes=64)
+            else:
+                c = work.tile([P, 512], U32, name="wc%d" % q, tag="wc", bufs=12, align_bytes=64)
+                s = work.tile([P, 512], U8, name="ws%d" % q, tag="ws", bufs=12, align_bytes=64)
+            nc.vector.quantize_mx(out=c[:].bitcast(E5 if q < NT else E4), scales=s[:], in_=grp[q][:])
+            codes[q], scl[q] = c, s
+
+        def bias_matmul(i):
+            j, t = i // NT, i % NT
+            acc = acp.tile([P, 512], F32, name="dacc%d" % i, tag="acc", bufs=4)
+            nc.tensor.matmul(out=acc[:], lhsT=lperm[:, t, :], rhs=rrows[:, 512 * j : 512 * (j + 1)], start=True, stop=True)
+            accs[("d", i)] = acc
+
+        def bias_evac(i):
+            d = work.tile([P, 512], F32, name="d%d" % i, tag="d%d" % i, bufs=1, align_bytes=64)
+            cp(DEVAC[i], d[:], accs[("d", i)][:])
+            dtile[i] = d
+
+        def mx_group(m, t):
+            acc = acp.tile([P, 512], F32, name="acc%d_%d" % (m, t), tag="acc", bufs=4)
+            for g in range(NG):
+                q = 4 * m + g
+                nc.tensor.matmul_mx(
+                    out=acc[:],
+                    lhsT=codes[t][:, P * g : P * (g + 1)].bitcast(E5),
+                    lhsT_scale=scl[t][:, P * g : P * (g + 1)],
+                    rhs=codes[q][:].bitcast(E4),
+                    rhs_scale=scl[q][:],
+                    start=(g == 0),
+                    stop=(g == NG - 1),
+                )
+            accs[(m, t)] = acc
+
+        def epilogue(m, t):
+            j = (m - 1) // 2
+            d = dtile[NT * j + t]
+            if (m - 1) % 2 == 0:
+                nc.vector.tensor_tensor(out=d[:], in0=accs[(m, t)][:], in1=d[:], op=ALU.subtract)
+            else:
+                nc.vector.scalar_tensor_tensor(
+                    out=d[:], in0=accs[(m, t)][:], scalar=nlr[:, t : t + 1], in1=d[:], op0=ALU.mult, op1=ALU.add
+                )
+                nc.sync.dma_start(out=out_v[:, t, 512 * j : 512 * (j + 1)], in_=d[:])
+
+        with tc.manual_schedule():
+            nxt = NT + RAW_BUFS
+            for s in range(-LEAD, NSTEP + 2):
+                if 0 <= s < NSTEP:
+                    transposes(2 * s)
+                    transposes(2 * s + 1)
+                ds = [i for i in range(16) if DSTEP[i] == s]
+                for i in ds:
+                    bias_matmul(i)
+                groups = []
+                if s >= 4:
+                    m = (s - 2) // 2
+                    groups = [(m, 2 * (s % 2)), (m, 2 * (s % 2) + 1)]
+                for m, t in groups:
+                    mx_group(m, t)
+
+                ahead = [q for q in (2 * (s + LEAD), 2 * (s + LEAD) + 1) if 0 <= q < NUNIT]
+                sh_v = [q for q in ahead if SHUF[q] != "S"]
+                sh_s = [q for q in ahead if SHUF[q] == "S"]
+                tr = 0 <= s < NSTEP
+                if s >= HEADN:
+                    for q in sh_v[:1]:
+                        shuffle(q)
+                if tr:
+                    evacuate(2 * s, 0, EVAC[(s, 0)])
+                    evacuate(2 * s, 1, EVAC[(s, 1)])
+                    quantize(2 * s)
+                if s >= HEADN:
+                    for q in sh_v[1:]:
+                        shuffle(q)
+                if tr:
+                    evacuate(2 * s + 1, 0, EVAC[(s, 2)])
+                    evacuate(2 * s + 1, 1, EVAC[(s, 3)])
+                    quantize(2 * s + 1)
+                for i in ds:
+                    bias_evac(i)
+                if s < HEADN:
+                    for q in sh_v:
+                        shuffle(q)
+                for q in sh_s:
+                    shuffle(q)
+                for m, t in groups:
+                    epilogue(m, t)
+                if s >= 2 and nxt < NLOAD:
+                    load(nxt)
+                    nxt += 1

@@ -17,21 +17,24 @@ ALU = mybir.AluOpType
 P = 128
 NT = 4
 NJ = 4
-NG = 4
-NUNIT = 36
-NSTEP = NUNIT // 2
+NSTEP = 18
 RAW_BUFS = 8
-
-LEAD = 2
-HEADN = 6
+SH_BUFS = 6
+NWARM = 3
 
 
 def tile_optimizedlinear_kernel(tc, input_data, weight, bias, prev_grad, prev_bias_grad, lr_samples, out):
     nc = tc.nc
-    SHUF = {q: (None if q < 8 else "V" if q % 4 != 3 else "S") for q in range(NUNIT)}
-    EVAC = {(s, i): ("V" if (s < 4 and i % 2 == 1) else "S") for s in range(NSTEP) for i in range(4)}
-    DSTEP = {i: i for i in range(16)}
-    DEVAC = {i: "S" for i in range(16)}
+    HT = [("x", 0, 0), ("w", 0, 0), ("x", 0, 1), ("w", 0, 1), ("g", 0, 0), ("g", 0, 1)]
+    for j in range(1, NJ):
+        HT.extend([("w", j, 0), ("w", j, 1), ("g", j, 0), ("g", j, 1)])
+    SHUF = {(s, gl): (None if s < 4 else "V") for s in range(NSTEP) for gl in range(2)}
+    for s in range(7, NSTEP, 2):
+        SHUF[(s + 1, 1)] = "S"
+    EVAC = {(s, i): "S" for s in range(NSTEP) for i in range(4)}
+    DEVAC = {i: ("V" if i < 4 else "S") for i in range(16)}
+    KEEP = {1: 2}
+
     x_v = input_data.rearrange("(p t) k -> p t k", t=NT)
     out_v = out.rearrange("(p t) o -> p t o", t=NT)
 
@@ -42,12 +45,14 @@ def tile_optimizedlinear_kernel(tc, input_data, weight, bias, prev_grad, prev_bi
         tps = ctx.enter_context(tc.psum_pool(name="tps", bufs=4))
         acp = ctx.enter_context(tc.psum_pool(name="acp", bufs=4))
 
-        def cp(who, dst, src):
+        def cp(who, dst, frm):
             if who == "V":
-                nc.vector.tensor_copy(out=dst, in_=src)
+                nc.vector.tensor_copy(out=dst, in_=frm)
             else:
-                nc.scalar.copy(out=dst, in_=src)
+                nc.scalar.copy(out=dst, in_=frm)
 
+        zeros = const.tile([P, 512], F32, name="zeros")
+        nc.vector.memset(zeros[:], 0.0)
         ident = const.tile([P, P], F32, name="ident")
         make_identity(nc, ident[:])
         rrows = const.tile([P, OUT], BF16, name="rrows")
@@ -58,79 +63,80 @@ def tile_optimizedlinear_kernel(tc, input_data, weight, bias, prev_grad, prev_bi
         nc.vector.memset(lrows[:], 0.0)
         nc.vector.memset(lrows[0:1, :], -1.0)
         nc.vector.memset(rrows[:], 0.0)
-        nc.scalar.dma_start(out=lrows[1:2, :], in_=lr_samples.rearrange("(o n) -> o n", o=1))
-        nc.scalar.dma_start(out=rrows[0:1, :], in_=bias.rearrange("(o n) -> o n", o=1))
-        nc.scalar.dma_start(out=rrows[1:2, :], in_=prev_bias_grad.rearrange("(o n) -> o n", o=1))
-        nc.scalar.dma_start(out=lr_pt[:], in_=lr_samples.rearrange("(p t) -> p t", t=NT))
 
         raw = {}
 
-        def load(d):
-            if d < NT:
-                r = rawp.tile([P, IN], BF16, name="xr%d" % d, tag="xr", bufs=NT, align_bytes=64)
-                nc.sync.dma_start(out=r[:], in_=x_v[:, d, :])
+        def load(s):
+            mat, j, kh = HT[s]
+            r = rawp.tile([P, 4, IN // 2], BF16, name="raw%d" % s, tag="raw", bufs=RAW_BUFS, align_bytes=64)
+            ks = slice(1024 * kh, 1024 * (kh + 1))
+            if mat == "x":
+                nc.sync.dma_start(out=r[:], in_=x_v[:, :, ks])
             else:
-                i = d - NT
-                mat = weight if (i // 2) % 2 == 0 else prev_grad
-                j, h = i // 4, i % 2
-                r = rawp.tile([P, 4, IN // 2], BF16, name="wr%d" % i, tag="wr", bufs=RAW_BUFS, align_bytes=64)
-                nc.sync.dma_start(
-                    out=r[:],
-                    in_=mat[512 * j : 512 * (j + 1), 1024 * h : 1024 * (h + 1)].rearrange("(a r) k -> r a k", a=4),
-                )
-            raw[d] = r
+                m_ap = weight if mat == "w" else prev_grad
+                nc.sync.dma_start(out=r[:], in_=m_ap[512 * j : 512 * (j + 1), ks].rearrange("(a r) k -> r a k", a=4))
+            raw[s] = r
 
-        NLOAD = NT + 16
-        for d in range(NT + RAW_BUFS):
-            load(d)
+        load(0)
+        nc.sync.dma_start(out=lrows[1:2, :], in_=lr_samples.rearrange("(o n) -> o n", o=1))
+        nc.sync.dma_start(out=rrows[0:1, :], in_=bias.rearrange("(o n) -> o n", o=1))
+        nc.sync.dma_start(out=rrows[1:2, :], in_=prev_bias_grad.rearrange("(o n) -> o n", o=1))
+        nc.sync.dma_start(out=lr_pt[:], in_=lr_samples.rearrange("(p t) -> p t", t=NT))
+        for s in range(1, RAW_BUFS):
+            load(s)
 
-        nc.vector.tensor_copy(out=lperm[:], in_=lrows[:].rearrange("p (m t) -> p t m", t=NT))
-        nc.vector.tensor_scalar(out=nlr[:], in0=lr_pt[:], scalar1=-1.0, scalar2=None, op0=ALU.mult)
-
-        def unit_words(q):
-            if q < NT:
-                return raw[q][:].bitcast(F32).rearrange("p (a w u) -> p a u w", a=4, u=2)
-            i, gl = (q - NT) // 2, q % 2
-            return raw[NT + i][:].bitcast(F32)[:, :, 256 * gl : 256 * (gl + 1)].rearrange("p a (w u) -> p a u w", u=2)
-
-        src = {}
+        words = {}
         banks = {}
         grp = {}
         codes = {}
         scl = {}
+        xcodes = {}
+        xscl = {}
         dtile = {}
         accs = {}
 
-        def shuffle(q):
-            if SHUF[q] is None:
-                src[q] = unit_words(q)
+        def shuffle(s, gl):
+            v = raw[s][:].bitcast(F32)[:, :, 256 * gl : 256 * (gl + 1)].rearrange("p a (w u) -> p a u w", u=2)
+            if SHUF[(s, gl)] is None:
+                words[(s, gl)] = v
                 return
-            s = work.tile([P, 4, 2, P], F32, name="sh%d" % q, tag="sh", bufs=2 * LEAD + 2, align_bytes=64)
-            cp(SHUF[q], s[:], unit_words(q))
-            src[q] = s[:]
+            sh = work.tile([P, 4, 2, P], F32, name="sh%d_%d" % (s, gl), tag="sh", bufs=SH_BUFS, align_bytes=64)
+            cp(SHUF[(s, gl)], sh[:], v)
+            words[(s, gl)] = sh[:]
 
-        def transposes(q):
+        def transposes(s, gl):
             for h in range(2):
-                bk = tps.tile([P, 4, P], F32, name="tb%d_%d" % (q, h), tag="tb", bufs=4)
-                banks[(q, h)] = bk
+                bk = tps.tile([P, 4, P], F32, name="tb%d_%d_%d" % (s, gl, h), tag="tb", bufs=4)
+                banks[(s, gl, h)] = bk
                 for i in range(4):
-                    nc.tensor.transpose(out=bk[:, i, :], in_=src[q][:, 2 * h + i // 2, i % 2, :], identity=ident[:])
+                    nc.tensor.transpose(out=bk[:, i, :], in_=words[(s, gl)][:, 2 * h + i // 2, i % 2, :], identity=ident[:])
 
-        def evacuate(q, h, who):
+        def evacuate(s, gl, h):
             if h == 0:
-                grp[q] = work.tile([P, 4 * 512], BF16, name="gr%d" % q, tag="gr", bufs=4, align_bytes=64)
-            dst = grp[q][:].bitcast(F32).rearrange("p (a r u) -> p a r u", a=4, u=2)[:, 2 * h : 2 * h + 2, :, :]
-            cp(who, dst, banks[(q, h)][:].rearrange("p (a u) r -> p a r u", u=2))
+                grp[(s, gl)] = work.tile([P, 4 * 512], BF16, name="gr%d_%d" % (s, gl), tag="gr", bufs=4, align_bytes=64)
+            dst = grp[(s, gl)][:].bitcast(F32).rearrange("p (a r u) -> p a r u", a=4, u=2)[:, 2 * h : 2 * h + 2, :, :]
+            cp(EVAC[(s, 2 * gl + h)], dst, banks[(s, gl, h)][:].rearrange("p (a u) r -> p a r u", u=2))
 
-        def quantize(q):
-            if q < NT:
-                c = work.tile([P, 512], U32, name="xc%d" % q, tag="xc", bufs=NT, align_bytes=64)
-                s = work.tile([P, 512], U8, name="xs%d" % q, tag="xs", bufs=NT, align_bytes=64)
+        def quantize(s, gl):
+            mat, j, kh = HT[s]
+            if mat == "x":
+                c = work.tile([P, 512], U32, name="xc%d_%d" % (s, gl), tag="xc", bufs=4, align_bytes=64)
+                sc = work.tile([P, 512], U8, name="xs%d_%d" % (s, gl), tag="xs", bufs=4, align_bytes=64)
+                xcodes[2 * kh + gl], xscl[2 * kh + gl] = c, sc
             else:
-                c = work.tile([P, 512], U32, name="wc%d" % q, tag="wc", bufs=12, align_bytes=64)
-                s = work.tile([P, 512], U8, name="ws%d" % q, tag="ws", bufs=12, align_bytes=64)
-            nc.vector.quantize_mx(out=c[:].bitcast(E5 if q < NT else E4), scales=s[:], in_=grp[q][:])
-            codes[q], scl[q] = c, s
+                c = work.tile([P, 512], U32, name="wc%d_%d" % (s, gl), tag="wc", bufs=8, align_bytes=64)
+                sc = work.tile([P, 512], U8, name="ws%d_%d" % (s, gl), tag="ws", bufs=8, align_bytes=64)
+                codes[(s, gl)], scl[(s, gl)] = c, sc
+            nc.vector.quantize_mx(out=c[:].bitcast(E5 if mat == "x" else E4), scales=sc[:], in_=grp[(s, gl)][:])
+
+        def warm(n, wide):
+            junk = acp.tile([P, 512], F32, name="junk", tag="acc", bufs=4)
+            for i in range(n):
+                if wide:
+                    nc.tensor.matmul(out=junk[:], lhsT=zeros[:, 0:P], rhs=zeros[:], start=True, stop=True)
+                else:
+                    zb = zeros[:].bitcast(BF16)
+                    nc.tensor.matmul(out=junk[:], lhsT=zb[:, 0:P], rhs=zb[:, 0:512], start=True, stop=True)
 
         def bias_matmul(i):
             j, t = i // NT, i % NT
@@ -143,75 +149,93 @@ def tile_optimizedlinear_kernel(tc, input_data, weight, bias, prev_grad, prev_bi
             cp(DEVAC[i], d[:], accs[("d", i)][:])
             dtile[i] = d
 
-        def mx_group(m, t):
-            acc = acp.tile([P, 512], F32, name="acc%d_%d" % (m, t), tag="acc", bufs=4)
-            for g in range(NG):
-                q = 4 * m + g
-                nc.tensor.matmul_mx(
-                    out=acc[:],
-                    lhsT=codes[t][:, P * g : P * (g + 1)].bitcast(E5),
-                    lhsT_scale=scl[t][:, P * g : P * (g + 1)],
-                    rhs=codes[q][:].bitcast(E4),
-                    rhs_scale=scl[q][:],
-                    start=(g == 0),
-                    stop=(g == NG - 1),
-                )
-            accs[(m, t)] = acc
+        def mx_run(s):
+            mat, j, kh = HT[s]
+            for t in range(NT):
+                if kh == 0:
+                    accs[(mat, j, t)] = acp.tile([P, 512], F32, name="acc%s%d_%d" % (mat, j, t), tag="acc", bufs=4)
+                for gl in range(2):
+                    g = 2 * kh + gl
+                    nc.tensor.matmul_mx(
+                        out=accs[(mat, j, t)][:],
+                        lhsT=xcodes[g][:, P * t : P * (t + 1)].bitcast(E5),
+                        lhsT_scale=xscl[g][:, P * t : P * (t + 1)],
+                        rhs=codes[(s, gl)][:].bitcast(E4),
+                        rhs_scale=scl[(s, gl)][:],
+                        start=(g == 0),
+                        stop=(g == 3),
+                    )
 
-        def epilogue(m, t):
-            j = (m - 1) // 2
+        def epilogue(s, t):
+            mat, j, kh = HT[s]
             d = dtile[NT * j + t]
-            if (m - 1) % 2 == 0:
-                nc.vector.tensor_tensor(out=d[:], in0=accs[(m, t)][:], in1=d[:], op=ALU.subtract)
+            if mat == "w":
+                nc.vector.tensor_tensor(out=d[:], in0=accs[(mat, j, t)][:], in1=d[:], op=ALU.subtract)
             else:
                 nc.vector.scalar_tensor_tensor(
-                    out=d[:], in0=accs[(m, t)][:], scalar=nlr[:, t : t + 1], in1=d[:], op0=ALU.mult, op1=ALU.add
+                    out=d[:], in0=accs[(mat, j, t)][:], scalar=nlr[:, t : t + 1], in1=d[:], op0=ALU.mult, op1=ALU.add
                 )
                 nc.sync.dma_start(out=out_v[:, t, 512 * j : 512 * (j + 1)], in_=d[:])
 
-        with tc.manual_schedule():
-            nxt = NT + RAW_BUFS
-            for s in range(-LEAD, NSTEP + 2):
-                if 0 <= s < NSTEP:
-                    transposes(2 * s)
-                    transposes(2 * s + 1)
-                ds = [i for i in range(16) if DSTEP[i] == s]
-                for i in ds:
-                    bias_matmul(i)
-                groups = []
-                if s >= 4:
-                    m = (s - 2) // 2
-                    groups = [(m, 2 * (s % 2)), (m, 2 * (s % 2) + 1)]
-                for m, t in groups:
-                    mx_group(m, t)
+        plan = {s: [] for s in range(-1, NSTEP + 1)}
+        for s in range(-1, 5):
+            plan[s] = [(s + 1, 0), (s + 1, 1)]
+        for s in range(5, NSTEP, 2):
+            plan[s] = [(s2, gl) for s2 in (s + 1, s + 2) if s2 < NSTEP for gl in range(2)]
 
-                ahead = [q for q in (2 * (s + LEAD), 2 * (s + LEAD) + 1) if 0 <= q < NUNIT]
-                sh_v = [q for q in ahead if SHUF[q] != "S"]
-                sh_s = [q for q in ahead if SHUF[q] == "S"]
+        with tc.manual_schedule():
+            warm(NWARM, True)
+            for s in range(-1, NSTEP + 1):
                 tr = 0 <= s < NSTEP
-                if s >= HEADN:
-                    for q in sh_v[:1]:
-                        shuffle(q)
                 if tr:
-                    evacuate(2 * s, 0, EVAC[(s, 0)])
-                    evacuate(2 * s, 1, EVAC[(s, 1)])
-                    quantize(2 * s)
-                if s >= HEADN:
-                    for q in sh_v[1:]:
-                        shuffle(q)
+                    transposes(s, 0)
+                    transposes(s, 1)
+                if s in KEEP:
+                    warm(KEEP[s], False)
+                run = s - 1 if (s >= 2 and HT[s - 1][0] != "x") else None
+                closing = run is not None and HT[run][2] == 1
+                ds = []
+                if run is not None:
+                    mx_run(run)
+                    if closing and HT[run][1] + 1 < NJ:
+                        i0 = NT * (HT[run][1] + 1) + (0 if HT[run][0] == "w" else 2)
+                        ds = [i0, i0 + 1]
+                        for i in ds:
+                            bias_matmul(i)
+                if s == 0:
+                    ds = [0, 1, 2, 3]
+                    for i in ds:
+                        bias_matmul(i)
+
+                sh_v = [u for u in plan[s] if SHUF[u] != "S"]
+                sh_s = [u for u in plan[s] if SHUF[u] == "S"]
+                eps = [0, 1, 2, 3] if closing else []
+                early = True
+                if early:
+                    for u in sh_v[:1]:
+                        shuffle(u[0], u[1])
                 if tr:
-                    evacuate(2 * s + 1, 0, EVAC[(s, 2)])
-                    evacuate(2 * s + 1, 1, EVAC[(s, 3)])
-                    quantize(2 * s + 1)
+                    evacuate(s, 0, 0)
+                    evacuate(s, 0, 1)
+                    quantize(s, 0)
+                for t in eps[:1]:
+                    epilogue(run, t)
+                for u in sh_v[1:2] if early else sh_v[:2]:
+                    shuffle(u[0], u[1])
+                if tr:
+                    evacuate(s, 1, 0)
+                    evacuate(s, 1, 1)
+                    quantize(s, 1)
+                for t in eps[1:]:
+                    epilogue(run, t)
+                for u in sh_v[2:]:
+                    shuffle(u[0], u[1])
+                if s == -1:
+                    nc.vector.tensor_copy(out=lperm[:], in_=lrows[:].rearrange("p (m t) -> p t m", t=NT))
+                    nc.vector.tensor_scalar(out=nlr[:], in0=lr_pt[:], scalar1=-1.0, scalar2=None, op0=ALU.mult)
                 for i in ds:
                     bias_evac(i)
-                if s < HEADN:
-                    for q in sh_v:
-                        shuffle(q)
-                for q in sh_s:
-                    shuffle(q)
-                for m, t in groups:
-                    epilogue(m, t)
-                if s >= 2 and nxt < NLOAD:
-                    load(nxt)
-                    nxt += 1
+                for u in sh_s:
+                    shuffle(u[0], u[1])
+                if tr and s + RAW_BUFS < NSTEP:
+                    load(s + RAW_BUFS)

@@ -17,24 +17,21 @@ ALU = mybir.AluOpType
 P = 128
 NT = 4
 NJ = 4
-NSTEP = 18
+NG = 4
+NUNIT = 36
+NSTEP = NUNIT // 2
 RAW_BUFS = 8
-SH_BUFS = 6
-NWARM = 3
+
+LEAD = 2
+HEADN = 6
 
 
 def tile_optimizedlinear_kernel(tc, input_data, weight, bias, prev_grad, prev_bias_grad, lr_samples, out):
     nc = tc.nc
-    HT = [("x", 0, 0), ("w", 0, 0), ("x", 0, 1), ("w", 0, 1), ("g", 0, 0), ("g", 0, 1)]
-    for j in range(1, NJ):
-        HT.extend([("w", j, 0), ("w", j, 1), ("g", j, 0), ("g", j, 1)])
-    SHUF = {(s, gl): (None if s < 4 else "V") for s in range(NSTEP) for gl in range(2)}
-    for s in range(7, NSTEP, 2):
-        SHUF[(s + 1, 1)] = "S"
-    EVAC = {(s, i): "S" for s in range(NSTEP) for i in range(4)}
-    DEVAC = {i: ("V" if i < 4 else "S") for i in range(16)}
-    KEEP = {1: 2}
-
+    SHUF = {q: (None if q < 12 else "V" if q % 4 != 3 else "S") for q in range(NUNIT)}
+    EVAC = {(s, i): ("V" if (s < 4 and i % 2 == 1) else "S") for s in range(NSTEP) for i in range(4)}
+    DSTEP = {i: i for i in range(16)}
+    DEVAC = {i: "S" for i in range(16)}
     x_v = input_data.rearrange("(p t) k -> p t k", t=NT)
     out_v = out.rearrange("(p t) o -> p t o", t=NT)
 
@@ -45,14 +42,12 @@ def tile_optimizedlinear_kernel(tc, input_data, weight, bias, prev_grad, prev_bi
         tps = ctx.enter_context(tc.psum_pool(name="tps", bufs=4))
         acp = ctx.enter_context(tc.psum_pool(name="acp", bufs=4))
 
-        def cp(who, dst, frm):
+        def cp(who, dst, src):
             if who == "V":
-                nc.vector.tensor_copy(out=dst, in_=frm)
+                nc.vector.tensor_copy(out=dst, in_=src)
             else:
-                nc.scalar.copy(out=dst, in_=frm)
+                nc.scalar.copy(out=dst, in_=src)
 
-        zeros = const.tile([P, 512], F32, name="zeros")
-        nc.vector.memset(zeros[:], 0.0)
         ident = const.tile([P, P], F32, name="ident")
         make_identity(nc, ident[:])
         rrows = const.tile([P, OUT], BF16, name="rrows")
@@ -66,77 +61,77 @@ def tile_optimizedlinear_kernel(tc, input_data, weight, bias, prev_grad, prev_bi
 
         raw = {}
 
-        def load(s):
-            mat, j, kh = HT[s]
-            r = rawp.tile([P, 4, IN // 2], BF16, name="raw%d" % s, tag="raw", bufs=RAW_BUFS, align_bytes=64)
-            ks = slice(1024 * kh, 1024 * (kh + 1))
-            if mat == "x":
-                nc.sync.dma_start(out=r[:], in_=x_v[:, :, ks])
+        def load(d):
+            if d < NT:
+                r = rawp.tile([P, IN], BF16, name="xr%d" % d, tag="xr", bufs=NT, align_bytes=64)
+                nc.sync.dma_start(out=r[:], in_=x_v[:, d, :])
             else:
-                m_ap = weight if mat == "w" else prev_grad
-                nc.sync.dma_start(out=r[:], in_=m_ap[512 * j : 512 * (j + 1), ks].rearrange("(a r) k -> r a k", a=4))
-            raw[s] = r
+                i = d - NT
+                mat = weight if (i // 2) % 2 == 0 else prev_grad
+                j, h = i // 4, i % 2
+                r = rawp.tile([P, 4, IN // 2], BF16, name="wr%d" % i, tag="wr", bufs=RAW_BUFS, align_bytes=64)
+                nc.sync.dma_start(
+                    out=r[:],
+                    in_=mat[512 * j : 512 * (j + 1), 1024 * h : 1024 * (h + 1)].rearrange("(a r) k -> r a k", a=4),
+                )
+            raw[d] = r
 
+        NLOAD = NT + 16
         load(0)
         nc.sync.dma_start(out=lrows[1:2, :], in_=lr_samples.rearrange("(o n) -> o n", o=1))
         nc.sync.dma_start(out=rrows[0:1, :], in_=bias.rearrange("(o n) -> o n", o=1))
         nc.sync.dma_start(out=rrows[1:2, :], in_=prev_bias_grad.rearrange("(o n) -> o n", o=1))
         nc.sync.dma_start(out=lr_pt[:], in_=lr_samples.rearrange("(p t) -> p t", t=NT))
-        for s in range(1, RAW_BUFS):
-            load(s)
+        for d in range(1, NT + RAW_BUFS):
+            load(d)
 
-        words = {}
+        nc.vector.tensor_copy(out=lperm[:], in_=lrows[:].rearrange("p (m t) -> p t m", t=NT))
+        nc.vector.tensor_scalar(out=nlr[:], in0=lr_pt[:], scalar1=-1.0, scalar2=None, op0=ALU.mult)
+
+        def unit_words(q):
+            if q < NT:
+                return raw[q][:].bitcast(F32).rearrange("p (a w u) -> p a u w", a=4, u=2)
+            i, gl = (q - NT) // 2, q % 2
+            return raw[NT + i][:].bitcast(F32)[:, :, 256 * gl : 256 * (gl + 1)].rearrange("p a (w u) -> p a u w", u=2)
+
+        src = {}
         banks = {}
         grp = {}
         codes = {}
         scl = {}
-        xcodes = {}
-        xscl = {}
         dtile = {}
         accs = {}
 
-        def shuffle(s, gl):
-            v = raw[s][:].bitcast(F32)[:, :, 256 * gl : 256 * (gl + 1)].rearrange("p a (w u) -> p a u w", u=2)
-            if SHUF[(s, gl)] is None:
-                words[(s, gl)] = v
+        def shuffle(q):
+            if SHUF[q] is None:
+                src[q] = unit_words(q)
                 return
-            sh = work.tile([P, 4, 2, P], F32, name="sh%d_%d" % (s, gl), tag="sh", bufs=SH_BUFS, align_bytes=64)
-            cp(SHUF[(s, gl)], sh[:], v)
-            words[(s, gl)] = sh[:]
+            s = work.tile([P, 4, 2, P], F32, name="sh%d" % q, tag="sh", bufs=2 * LEAD + 2, align_bytes=64)
+            cp(SHUF[q], s[:], unit_words(q))
+            src[q] = s[:]
 
-        def transposes(s, gl):
+        def transposes(q):
             for h in range(2):
-                bk = tps.tile([P, 4, P], F32, name="tb%d_%d_%d" % (s, gl, h), tag="tb", bufs=4)
-                banks[(s, gl, h)] = bk
+                bk = tps.tile([P, 4, P], F32, name="tb%d_%d" % (q, h), tag="tb", bufs=4)
+                banks[(q, h)] = bk
                 for i in range(4):
-                    nc.tensor.transpose(out=bk[:, i, :], in_=words[(s, gl)][:, 2 * h + i // 2, i % 2, :], identity=ident[:])
+                    nc.tensor.transpose(out=bk[:, i, :], in_=src[q][:, 2 * h + i // 2, i % 2, :], identity=ident[:])
 
-        def evacuate(s, gl, h):
+        def evacuate(q, h, who):
             if h == 0:
-                grp[(s, gl)] = work.tile([P, 4 * 512], BF16, name="gr%d_%d" % (s, gl), tag="gr", bufs=4, align_bytes=64)
-            dst = grp[(s, gl)][:].bitcast(F32).rearrange("p (a r u) -> p a r u", a=4, u=2)[:, 2 * h : 2 * h + 2, :, :]
-            cp(EVAC[(s, 2 * gl + h)], dst, banks[(s, gl, h)][:].rearrange("p (a u) r -> p a r u", u=2))
+                grp[q] = work.tile([P, 4 * 512], BF16, name="gr%d" % q, tag="gr", bufs=4, align_bytes=64)
+            dst = grp[q][:].bitcast(F32).rearrange("p (a r u) -> p a r u", a=4, u=2)[:, 2 * h : 2 * h + 2, :, :]
+            cp(who, dst, banks[(q, h)][:].rearrange("p (a u) r -> p a r u", u=2))
 
-        def quantize(s, gl):
-            mat, j, kh = HT[s]
-            if mat == "x":
-                c = work.tile([P, 512], U32, name="xc%d_%d" % (s, gl), tag="xc", bufs=4, align_bytes=64)
-                sc = work.tile([P, 512], U8, name="xs%d_%d" % (s, gl), tag="xs", bufs=4, align_bytes=64)
-                xcodes[2 * kh + gl], xscl[2 * kh + gl] = c, sc
+        def quantize(q):
+            if q < NT:
+                c = work.tile([P, 512], U32, name="xc%d" % q, tag="xc", bufs=NT, align_bytes=64)
+                s = work.tile([P, 512], U8, name="xs%d" % q, tag="xs", bufs=NT, align_bytes=64)
             else:
-                c = work.tile([P, 512], U32, name="wc%d_%d" % (s, gl), tag="wc", bufs=8, align_bytes=64)
-                sc = work.tile([P, 512], U8, name="ws%d_%d" % (s, gl), tag="ws", bufs=8, align_bytes=64)
-                codes[(s, gl)], scl[(s, gl)] = c, sc
-            nc.vector.quantize_mx(out=c[:].bitcast(E5 if mat == "x" else E4), scales=sc[:], in_=grp[(s, gl)][:])
-
-        def warm(n, wide):
-            junk = acp.tile([P, 512], F32, name="junk", tag="acc", bufs=4)
-            for i in range(n):
-                if wide:
-                    nc.tensor.matmul(out=junk[:], lhsT=zeros[:, 0:P], rhs=zeros[:], start=True, stop=True)
-                else:
-                    zb = zeros[:].bitcast(BF16)
-                    nc.tensor.matmul(out=junk[:], lhsT=zb[:, 0:P], rhs=zb[:, 0:512], start=True, stop=True)
+                c = work.tile([P, 512], U32, name="wc%d" % q, tag="wc", bufs=12, align_bytes=64)
+                s = work.tile([P, 512], U8, name="ws%d" % q, tag="ws", bufs=12, align_bytes=64)
+            nc.vector.quantize_mx(out=c[:].bitcast(E5 if q < NT else E4), scales=s[:], in_=grp[q][:])
+            codes[q], scl[q] = c, s
 
         def bias_matmul(i):
             j, t = i // NT, i % NT
@@ -149,93 +144,75 @@ def tile_optimizedlinear_kernel(tc, input_data, weight, bias, prev_grad, prev_bi
             cp(DEVAC[i], d[:], accs[("d", i)][:])
             dtile[i] = d
 
-        def mx_run(s):
-            mat, j, kh = HT[s]
-            for t in range(NT):
-                if kh == 0:
-                    accs[(mat, j, t)] = acp.tile([P, 512], F32, name="acc%s%d_%d" % (mat, j, t), tag="acc", bufs=4)
-                for gl in range(2):
-                    g = 2 * kh + gl
-                    nc.tensor.matmul_mx(
-                        out=accs[(mat, j, t)][:],
-                        lhsT=xcodes[g][:, P * t : P * (t + 1)].bitcast(E5),
-                        lhsT_scale=xscl[g][:, P * t : P * (t + 1)],
-                        rhs=codes[(s, gl)][:].bitcast(E4),
-                        rhs_scale=scl[(s, gl)][:],
-                        start=(g == 0),
-                        stop=(g == 3),
-                    )
+        def mx_group(m, t):
+            acc = acp.tile([P, 512], F32, name="acc%d_%d" % (m, t), tag="acc", bufs=4)
+            for g in range(NG):
+                q = 4 * m + g
+                nc.tensor.matmul_mx(
+                    out=acc[:],
+                    lhsT=codes[t][:, P * g : P * (g + 1)].bitcast(E5),
+                    lhsT_scale=scl[t][:, P * g : P * (g + 1)],
+                    rhs=codes[q][:].bitcast(E4),
+                    rhs_scale=scl[q][:],
+                    start=(g == 0),
+                    stop=(g == NG - 1),
+                )
+            accs[(m, t)] = acc
 
-        def epilogue(s, t):
-            mat, j, kh = HT[s]
+        def epilogue(m, t):
+            j = (m - 1) // 2
             d = dtile[NT * j + t]
-            if mat == "w":
-                nc.vector.tensor_tensor(out=d[:], in0=accs[(mat, j, t)][:], in1=d[:], op=ALU.subtract)
+            if (m - 1) % 2 == 0:
+                nc.vector.tensor_tensor(out=d[:], in0=accs[(m, t)][:], in1=d[:], op=ALU.subtract)
             else:
                 nc.vector.scalar_tensor_tensor(
-                    out=d[:], in0=accs[(mat, j, t)][:], scalar=nlr[:, t : t + 1], in1=d[:], op0=ALU.mult, op1=ALU.add
+                    out=d[:], in0=accs[(m, t)][:], scalar=nlr[:, t : t + 1], in1=d[:], op0=ALU.mult, op1=ALU.add
                 )
                 nc.sync.dma_start(out=out_v[:, t, 512 * j : 512 * (j + 1)], in_=d[:])
 
-        plan = {s: [] for s in range(-1, NSTEP + 1)}
-        for s in range(-1, 5):
-            plan[s] = [(s + 1, 0), (s + 1, 1)]
-        for s in range(5, NSTEP, 2):
-            plan[s] = [(s2, gl) for s2 in (s + 1, s + 2) if s2 < NSTEP for gl in range(2)]
-
         with tc.manual_schedule():
-            warm(NWARM, True)
-            for s in range(-1, NSTEP + 1):
-                tr = 0 <= s < NSTEP
-                if tr:
-                    transposes(s, 0)
-                    transposes(s, 1)
-                if s in KEEP:
-                    warm(KEEP[s], False)
-                run = s - 1 if (s >= 2 and HT[s - 1][0] != "x") else None
-                closing = run is not None and HT[run][2] == 1
-                ds = []
-                if run is not None:
-                    mx_run(run)
-                    if closing and HT[run][1] + 1 < NJ:
-                        i0 = NT * (HT[run][1] + 1) + (0 if HT[run][0] == "w" else 2)
-                        ds = [i0, i0 + 1]
-                        for i in ds:
-                            bias_matmul(i)
-                if s == 0:
-                    ds = [0, 1, 2, 3]
-                    for i in ds:
-                        bias_matmul(i)
+            nxt = NT + RAW_BUFS
+            for s in range(-LEAD, NSTEP + 2):
+                if 0 <= s < NSTEP:
+                    transposes(2 * s)
+                    transposes(2 * s + 1)
+                ds = [i for i in range(16) if DSTEP[i] == s]
+                for i in ds:
+                    bias_matmul(i)
+                groups = []
+                if s >= 4:
+                    m = (s - 2) // 2
+                    groups = [(m, 2 * (s % 2)), (m, 2 * (s % 2) + 1)]
+                for m, t in groups:
+                    mx_group(m, t)
 
-                sh_v = [u for u in plan[s] if SHUF[u] != "S"]
-                sh_s = [u for u in plan[s] if SHUF[u] == "S"]
-                eps = [0, 1, 2, 3] if closing else []
-                early = True
-                if early:
-                    for u in sh_v[:1]:
-                        shuffle(u[0], u[1])
+                ahead = [q for q in (2 * (s + LEAD), 2 * (s + LEAD) + 1) if 0 <= q < NUNIT]
+                sh_v = [q for q in ahead if SHUF[q] != "S"]
+                sh_s = [q for q in ahead if SHUF[q] == "S"]
+                tr = 0 <= s < NSTEP
+                if s >= HEADN:
+                    for q in sh_v[:1]:
+                        shuffle(q)
                 if tr:
-                    evacuate(s, 0, 0)
-                    evacuate(s, 0, 1)
-                    quantize(s, 0)
-                for t in eps[:1]:
-                    epilogue(run, t)
-                for u in sh_v[1:2] if early else sh_v[:2]:
-                    shuffle(u[0], u[1])
+                    evacuate(2 * s, 0, EVAC[(s, 0)])
+                    evacuate(2 * s, 1, EVAC[(s, 1)])
+                    quantize(2 * s)
+                if s >= HEADN:
+                    for q in sh_v[1:]:
+                        shuffle(q)
                 if tr:
-                    evacuate(s, 1, 0)
-                    evacuate(s, 1, 1)
-                    quantize(s, 1)
-                for t in eps[1:]:
-                    epilogue(run, t)
-                for u in sh_v[2:]:
-                    shuffle(u[0], u[1])
-                if s == -1:
-                    nc.vector.tensor_copy(out=lperm[:], in_=lrows[:].rearrange("p (m t) -> p t m", t=NT))
-                    nc.vector.tensor_scalar(out=nlr[:], in0=lr_pt[:], scalar1=-1.0, scalar2=None, op0=ALU.mult)
+                    evacuate(2 * s + 1, 0, EVAC[(s, 2)])
+                    evacuate(2 * s + 1, 1, EVAC[(s, 3)])
+                    quantize(2 * s + 1)
                 for i in ds:
                     bias_evac(i)
-                for u in sh_s:
-                    shuffle(u[0], u[1])
-                if tr and s + RAW_BUFS < NSTEP:
-                    load(s + RAW_BUFS)
+                if s < HEADN:
+                    for q in sh_v:
+                        shuffle(q)
+                for q in sh_s:
+                    shuffle(q)
+                for m, t in groups:
+                    epilogue(m, t)
+                if s >= 2 and nxt < NLOAD:
+                    load(nxt)
+                    nxt += 1

@@ -23,7 +23,7 @@ NSTEP = NUNIT // 2
 RAW_BUFS = 8
 
 LEAD = 2
-HEADN = 6
+FINE = 6
 
 
 def tile_optimizedlinear_kernel(tc, input_data, weight, bias, prev_grad, prev_bias_grad, lr_samples, out):
@@ -39,8 +39,7 @@ def tile_optimizedlinear_kernel(tc, input_data, weight, bias, prev_grad, prev_bi
         const = ctx.enter_context(tc.tile_pool(name="const", bufs=1))
         rawp = ctx.enter_context(tc.tile_pool(name="rawp", bufs=1))
         work = ctx.enter_context(tc.tile_pool(name="work", bufs=1))
-        tps = ctx.enter_context(tc.psum_pool(name="tps", bufs=4))
-        acp = ctx.enter_context(tc.psum_pool(name="acp", bufs=4))
+        psp = ctx.enter_context(tc.psum_pool(name="psp", bufs=8))
 
         def cp(who, dst, src):
             if who == "V":
@@ -106,13 +105,13 @@ def tile_optimizedlinear_kernel(tc, input_data, weight, bias, prev_grad, prev_bi
             if SHUF[q] is None:
                 src[q] = unit_words(q)
                 return
-            s = work.tile([P, 4, 2, P], F32, name="sh%d" % q, tag="sh", bufs=2 * LEAD + 2, align_bytes=64)
+            s = work.tile([P, 4, 2, P], F32, name="sh%d" % q, tag="sh", bufs=8, align_bytes=64)
             cp(SHUF[q], s[:], unit_words(q))
             src[q] = s[:]
 
         def transposes(q):
             for h in range(2):
-                bk = tps.tile([P, 4, P], F32, name="tb%d_%d" % (q, h), tag="tb", bufs=4)
+                bk = psp.tile([P, 4, P], F32, name="tb%d_%d" % (q, h), tag="bk", bufs=8)
                 banks[(q, h)] = bk
                 for i in range(4):
                     nc.tensor.transpose(out=bk[:, i, :], in_=src[q][:, 2 * h + i // 2, i % 2, :], identity=ident[:])
@@ -135,7 +134,7 @@ def tile_optimizedlinear_kernel(tc, input_data, weight, bias, prev_grad, prev_bi
 
         def bias_matmul(i):
             j, t = i // NT, i % NT
-            acc = acp.tile([P, 512], F32, name="dacc%d" % i, tag="acc", bufs=4)
+            acc = psp.tile([P, 512], F32, name="dacc%d" % i, tag="bk", bufs=8)
             nc.tensor.matmul(out=acc[:], lhsT=lperm[:, t, :], rhs=rrows[:, 512 * j : 512 * (j + 1)], start=True, stop=True)
             accs[("d", i)] = acc
 
@@ -145,7 +144,7 @@ def tile_optimizedlinear_kernel(tc, input_data, weight, bias, prev_grad, prev_bi
             dtile[i] = d
 
         def mx_group(m, t):
-            acc = acp.tile([P, 512], F32, name="acc%d_%d" % (m, t), tag="acc", bufs=4)
+            acc = psp.tile([P, 512], F32, name="acc%d_%d" % (m, t), tag="bk", bufs=8)
             for g in range(NG):
                 q = 4 * m + g
                 nc.tensor.matmul_mx(
@@ -170,49 +169,57 @@ def tile_optimizedlinear_kernel(tc, input_data, weight, bias, prev_grad, prev_bi
                 )
                 nc.sync.dma_start(out=out_v[:, t, 512 * j : 512 * (j + 1)], in_=d[:])
 
+        RUNS = []
+        for s in range(FINE):
+            RUNS.append(([2 * s, 2 * s + 1], [s], [((s - 2) // 2, 2 * (s % 2) + e) for e in range(2)] if s >= 4 else []))
+        for s in range(FINE, NSTEP + 2, 2):
+            RUNS.append(
+                ([q for q in range(2 * s, 2 * s + 4) if q < NUNIT], [i for i in (s, s + 1) if i < 16], [((s - 2) // 2, t) for t in range(NT)])
+            )
+
         with tc.manual_schedule():
             nxt = NT + RAW_BUFS
-            for s in range(-LEAD, NSTEP + 2):
-                if 0 <= s < NSTEP:
-                    transposes(2 * s)
-                    transposes(2 * s + 1)
-                ds = [i for i in range(16) if DSTEP[i] == s]
+            done_sh = 0
+            for q in range(4):
+                shuffle(q)
+            done_sh = 4
+            for k in range(len(RUNS)):
+                units, ds, groups = RUNS[k]
+                for q in units:
+                    transposes(q)
                 for i in ds:
                     bias_matmul(i)
-                groups = []
-                if s >= 4:
-                    m = (s - 2) // 2
-                    groups = [(m, 2 * (s % 2)), (m, 2 * (s % 2) + 1)]
                 for m, t in groups:
                     mx_group(m, t)
-
-                ahead = [q for q in (2 * (s + LEAD), 2 * (s + LEAD) + 1) if 0 <= q < NUNIT]
+                ahead = []
+                target = min(NUNIT, (units[-1] + 1 if units else NUNIT) + 4)
+                while done_sh < target:
+                    ahead.append(done_sh)
+                    done_sh += 1
                 sh_v = [q for q in ahead if SHUF[q] != "S"]
                 sh_s = [q for q in ahead if SHUF[q] == "S"]
-                tr = 0 <= s < NSTEP
-                if s >= HEADN:
-                    for q in sh_v[:1]:
-                        shuffle(q)
-                if tr:
-                    evacuate(2 * s, 0, EVAC[(s, 0)])
-                    evacuate(2 * s, 1, EVAC[(s, 1)])
-                    quantize(2 * s)
-                if s >= HEADN:
-                    for q in sh_v[1:]:
-                        shuffle(q)
-                if tr:
-                    evacuate(2 * s + 1, 0, EVAC[(s, 2)])
-                    evacuate(2 * s + 1, 1, EVAC[(s, 3)])
-                    quantize(2 * s + 1)
+                eps = list(groups)
+                late = len(units) // 2
+                for n in range(len(units)):
+                    q = units[n]
+                    if len(units) == 4:
+                        for v in sh_v[n : n + 1]:
+                            shuffle(v)
+                    evacuate(q, 0, EVAC[(q // 2, 2 * (q % 2))])
+                    evacuate(q, 1, EVAC[(q // 2, 2 * (q % 2) + 1)])
+                    quantize(q)
+                    if n >= late and len(units) == 4 and eps:
+                        epilogue(eps[0][0], eps[0][1])
+                        eps = eps[1:]
                 for i in ds:
                     bias_evac(i)
-                if s < HEADN:
-                    for q in sh_v:
-                        shuffle(q)
-                for q in sh_s:
-                    shuffle(q)
-                for m, t in groups:
+                for v in sh_v[len(units) :] if len(units) == 4 else sh_v:
+                    shuffle(v)
+                for v in sh_s:
+                    shuffle(v)
+                for m, t in eps:
                     epilogue(m, t)
-                if s >= 2 and nxt < NLOAD:
-                    load(nxt)
-                    nxt += 1
+                for q in units:
+                    if q % 2 == 1 and q // 2 >= 2 and nxt < NLOAD:
+                        load(nxt)
+                        nxt += 1

@@ -20,7 +20,8 @@ NJ = 4
 NG = 4
 NUNIT = 36
 NSTEP = NUNIT // 2
-RAW_BUFS = 8
+RAW_BUFS = 6
+HL = 4
 
 LEAD = 2
 FINE = 6
@@ -68,11 +69,23 @@ def tile_optimizedlinear_kernel(tc, input_data, weight, bias, prev_grad, prev_bi
                 i = d - NT
                 mat = weight if (i // 2) % 2 == 0 else prev_grad
                 j, h = i // 4, i % 2
-                r = rawp.tile([P, 4, IN // 2], BF16, name="wr%d" % i, tag="wr", bufs=RAW_BUFS, align_bytes=64)
-                nc.sync.dma_start(
-                    out=r[:],
-                    in_=mat[512 * j : 512 * (j + 1), 1024 * h : 1024 * (h + 1)].rearrange("(a r) k -> r a k", a=4),
-                )
+                if i < HL:
+                    r = []
+                    for ah in range(2):
+                        rh = rawp.tile([P, 2, IN // 2], BF16, name="wh%d_%d" % (i, ah), tag="wh", bufs=2 * HL, align_bytes=64)
+                        nc.sync.dma_start(
+                            out=rh[:],
+                            in_=mat[512 * j + 256 * ah : 512 * j + 256 * (ah + 1), 1024 * h : 1024 * (h + 1)].rearrange(
+                                "(a r) k -> r a k", a=2
+                            ),
+                        )
+                        r.append(rh)
+                else:
+                    r = rawp.tile([P, 4, IN // 2], BF16, name="wr%d" % i, tag="wr", bufs=RAW_BUFS, align_bytes=64)
+                    nc.sync.dma_start(
+                        out=r[:],
+                        in_=mat[512 * j : 512 * (j + 1), 1024 * h : 1024 * (h + 1)].rearrange("(a r) k -> r a k", a=4),
+                    )
             raw[d] = r
 
         NLOAD = NT + 16
@@ -81,7 +94,7 @@ def tile_optimizedlinear_kernel(tc, input_data, weight, bias, prev_grad, prev_bi
         nc.sync.dma_start(out=rrows[0:1, :], in_=bias.rearrange("(o n) -> o n", o=1))
         nc.sync.dma_start(out=rrows[1:2, :], in_=prev_bias_grad.rearrange("(o n) -> o n", o=1))
         nc.sync.dma_start(out=lr_pt[:], in_=lr_samples.rearrange("(p t) -> p t", t=NT))
-        for d in range(1, NT + RAW_BUFS):
+        for d in range(1, NT + HL + RAW_BUFS):
             load(d)
 
         nc.vector.tensor_copy(out=lperm[:], in_=lrows[:].rearrange("p (m t) -> p t m", t=NT))
@@ -91,6 +104,10 @@ def tile_optimizedlinear_kernel(tc, input_data, weight, bias, prev_grad, prev_bi
             if q < NT:
                 return raw[q][:].bitcast(F32).rearrange("p (a w u) -> p a u w", a=4, u=2)
             i, gl = (q - NT) // 2, q % 2
+            if i < HL:
+                return [
+                    rh[:].bitcast(F32)[:, :, 256 * gl : 256 * (gl + 1)].rearrange("p a (w u) -> p a u w", u=2) for rh in raw[NT + i]
+                ]
             return raw[NT + i][:].bitcast(F32)[:, :, 256 * gl : 256 * (gl + 1)].rearrange("p a (w u) -> p a u w", u=2)
 
         src = {}
@@ -109,12 +126,19 @@ def tile_optimizedlinear_kernel(tc, input_data, weight, bias, prev_grad, prev_bi
             cp(SHUF[q], s[:], unit_words(q))
             src[q] = s[:]
 
+        def transposes_half(q, h):
+            bk = psp.tile([P, 4, P], F32, name="tb%d_%d" % (q, h), tag="bk", bufs=8)
+            banks[(q, h)] = bk
+            for i in range(4):
+                if isinstance(src[q], list):
+                    in_ = src[q][h][:, i // 2, i % 2, :]
+                else:
+                    in_ = src[q][:, 2 * h + i // 2, i % 2, :]
+                nc.tensor.transpose(out=bk[:, i, :], in_=in_, identity=ident[:])
+
         def transposes(q):
             for h in range(2):
-                bk = psp.tile([P, 4, P], F32, name="tb%d_%d" % (q, h), tag="bk", bufs=8)
-                banks[(q, h)] = bk
-                for i in range(4):
-                    nc.tensor.transpose(out=bk[:, i, :], in_=src[q][:, 2 * h + i // 2, i % 2, :], identity=ident[:])
+                transposes_half(q, h)
 
         def evacuate(q, h, who):
             if h == 0:
@@ -178,15 +202,21 @@ def tile_optimizedlinear_kernel(tc, input_data, weight, bias, prev_grad, prev_bi
             )
 
         with tc.manual_schedule():
-            nxt = NT + RAW_BUFS
+            nxt = NT + HL + RAW_BUFS
             done_sh = 0
             for q in range(4):
                 shuffle(q)
             done_sh = 4
             for k in range(len(RUNS)):
                 units, ds, groups = RUNS[k]
-                for q in units:
-                    transposes(q)
+                split = len(units) == 2 and NT <= units[0] < NT + 2 * HL
+                if split:
+                    for h in range(2):
+                        for q in units:
+                            transposes_half(q, h)
+                else:
+                    for q in units:
+                        transposes(q)
                 for i in ds:
                     bias_matmul(i)
                 for m, t in groups:
@@ -200,7 +230,13 @@ def tile_optimizedlinear_kernel(tc, input_data, weight, bias, prev_grad, prev_bi
                 sh_s = [q for q in ahead if SHUF[q] == "S"]
                 eps = list(groups)
                 late = len(units) // 2
-                for n in range(len(units)):
+                if split:
+                    for h in range(2):
+                        for n in range(2):
+                            evacuate(units[n], h, "V" if (units[0] // 2 < 4 and n == 1) else "S")
+                    for q in units:
+                        quantize(q)
+                for n in range(0 if split else len(units)):
                     q = units[n]
                     if len(units) == 4:
                         for v in sh_v[n : n + 1]:
@@ -220,6 +256,6 @@ def tile_optimizedlinear_kernel(tc, input_data, weight, bias, prev_grad, prev_bi
                 for m, t in eps:
                     epilogue(m, t)
                 for q in units:
-                    if q % 2 == 1 and q // 2 >= 2 and nxt < NLOAD:
+                    if q % 2 == 1 and q // 2 >= 2 + HL and nxt < NLOAD:
                         load(nxt)
                         nxt += 1

@@ -16,23 +16,19 @@ ALU = mybir.AluOpType
 
 P = 128
 NT = 4
-NJ = 4
 NG = 4
-NUNIT = 36
-NSTEP = NUNIT // 2
-RAW_BUFS = 6
+NPAIR = 18
+NBLK = 8
+RAW_BUFS = 5
 HL = 4
-
-LEAD = 2
+STRAIGHT = 6
 FINE = 6
 
 
 def tile_optimizedlinear_kernel(tc, input_data, weight, bias, prev_grad, prev_bias_grad, lr_samples, out):
     nc = tc.nc
-    SHUF = {q: (None if q < 12 else "V" if q % 4 != 3 else "S") for q in range(NUNIT)}
-    EVAC = {(s, i): ("V" if (s < 4 and i % 2 == 1) else "S") for s in range(NSTEP) for i in range(4)}
-    DSTEP = {i: i for i in range(16)}
-    DEVAC = {i: "S" for i in range(16)}
+    SHUF = {s: (None if s < STRAIGHT else "S" if s % 4 == 1 else "V") for s in range(NPAIR)}
+    EVAC = {(s, b): ("V" if (s < 4 and b in (1, 2)) else "S") for s in range(NPAIR) for b in range(4)}
     x_v = input_data.rearrange("(p t) k -> p t k", t=NT)
     out_v = out.rearrange("(p t) o -> p t o", t=NT)
 
@@ -42,11 +38,11 @@ def tile_optimizedlinear_kernel(tc, input_data, weight, bias, prev_grad, prev_bi
         work = ctx.enter_context(tc.tile_pool(name="work", bufs=1))
         psp = ctx.enter_context(tc.psum_pool(name="psp", bufs=8))
 
-        def cp(who, dst, src):
+        def cp(who, dst, src_ap):
             if who == "V":
-                nc.vector.tensor_copy(out=dst, in_=src)
+                nc.vector.tensor_copy(out=dst, in_=src_ap)
             else:
-                nc.scalar.copy(out=dst, in_=src)
+                nc.scalar.copy(out=dst, in_=src_ap)
 
         ident = const.tile([P, P], F32, name="ident")
         make_identity(nc, ident[:])
@@ -59,58 +55,52 @@ def tile_optimizedlinear_kernel(tc, input_data, weight, bias, prev_grad, prev_bi
         nc.vector.memset(lrows[0:1, :], -1.0)
         nc.vector.memset(rrows[:], 0.0)
 
-        raw = {}
+        xraw = {}
+        wraw = {}
 
-        def load(d):
-            if d < NT:
-                r = rawp.tile([P, IN], BF16, name="xr%d" % d, tag="xr", bufs=NT, align_bytes=64)
-                nc.sync.dma_start(out=r[:], in_=x_v[:, d, :])
-            else:
-                i = d - NT
-                mat = weight if (i // 2) % 2 == 0 else prev_grad
-                j, h = i // 4, i % 2
-                if i < HL:
-                    r = []
-                    for ah in range(2):
-                        rh = rawp.tile([P, 2, IN // 2], BF16, name="wh%d_%d" % (i, ah), tag="wh", bufs=2 * HL, align_bytes=64)
-                        nc.sync.dma_start(
-                            out=rh[:],
-                            in_=mat[512 * j + 256 * ah : 512 * j + 256 * (ah + 1), 1024 * h : 1024 * (h + 1)].rearrange(
-                                "(a r) k -> r a k", a=2
-                            ),
-                        )
-                        r.append(rh)
-                else:
-                    r = rawp.tile([P, 4, IN // 2], BF16, name="wr%d" % i, tag="wr", bufs=RAW_BUFS, align_bytes=64)
+        def load_x(t):
+            r = rawp.tile([P, IN], BF16, name="xr%d" % t, tag="xr", bufs=NT, align_bytes=64)
+            nc.sync.dma_start(out=r[:], in_=x_v[:, t, :])
+            xraw[t] = r
+
+        def load_w(i):
+            mat = weight if (i // 2) % 2 == 0 else prev_grad
+            j, h = i // 4, i % 2
+            if i < HL:
+                r = []
+                for ah in range(2):
+                    rh = rawp.tile([P, 2, IN // 2], BF16, name="wh%d_%d" % (i, ah), tag="wh", bufs=2 * HL, align_bytes=64)
                     nc.sync.dma_start(
-                        out=r[:],
-                        in_=mat[512 * j : 512 * (j + 1), 1024 * h : 1024 * (h + 1)].rearrange("(a r) k -> r a k", a=4),
+                        out=rh[:],
+                        in_=mat[512 * j + 256 * ah : 512 * j + 256 * (ah + 1), 1024 * h : 1024 * (h + 1)].rearrange(
+                            "(a r) k -> r a k", a=2
+                        ),
                     )
-            raw[d] = r
+                    r.append(rh)
+            else:
+                r = rawp.tile([P, 4, IN // 2], BF16, name="wr%d" % i, tag="wr", bufs=RAW_BUFS, align_bytes=64)
+                nc.sync.dma_start(
+                    out=r[:],
+                    in_=mat[512 * j : 512 * (j + 1), 1024 * h : 1024 * (h + 1)].rearrange("(a r) k -> r a k", a=4),
+                )
+            wraw[i] = r
 
-        NLOAD = NT + 16
-        load(0)
+        NLOAD = 16
+        load_x(0)
         nc.sync.dma_start(out=lrows[1:2, :], in_=lr_samples.rearrange("(o n) -> o n", o=1))
         nc.sync.dma_start(out=rrows[0:1, :], in_=bias.rearrange("(o n) -> o n", o=1))
         nc.sync.dma_start(out=rrows[1:2, :], in_=prev_bias_grad.rearrange("(o n) -> o n", o=1))
         nc.sync.dma_start(out=lr_pt[:], in_=lr_samples.rearrange("(p t) -> p t", t=NT))
-        for d in range(1, NT + HL + RAW_BUFS):
-            load(d)
+        for t in range(1, NT):
+            load_x(t)
+        for i in range(HL + RAW_BUFS):
+            load_w(i)
 
         nc.vector.tensor_copy(out=lperm[:], in_=lrows[:].rearrange("p (m t) -> p t m", t=NT))
         nc.vector.tensor_scalar(out=nlr[:], in0=lr_pt[:], scalar1=-1.0, scalar2=None, op0=ALU.mult)
 
-        def unit_words(q):
-            if q < NT:
-                return raw[q][:].bitcast(F32).rearrange("p (a w u) -> p a u w", a=4, u=2)
-            i, gl = (q - NT) // 2, q % 2
-            if i < HL:
-                return [
-                    rh[:].bitcast(F32)[:, :, 256 * gl : 256 * (gl + 1)].rearrange("p a (w u) -> p a u w", u=2) for rh in raw[NT + i]
-                ]
-            return raw[NT + i][:].bitcast(F32)[:, :, 256 * gl : 256 * (gl + 1)].rearrange("p a (w u) -> p a u w", u=2)
-
-        src = {}
+        nxt = [HL + RAW_BUFS]
+        shuf = {}
         banks = {}
         grp = {}
         codes = {}
@@ -118,43 +108,52 @@ def tile_optimizedlinear_kernel(tc, input_data, weight, bias, prev_grad, prev_bi
         dtile = {}
         accs = {}
 
-        def shuffle(q):
-            if SHUF[q] is None:
-                src[q] = unit_words(q)
-                return
-            s = work.tile([P, 4, 2, P], F32, name="sh%d" % q, tag="sh", bufs=8, align_bytes=64)
-            cp(SHUF[q], s[:], unit_words(q))
-            src[q] = s[:]
+        def bank_unit(s, b):
+            if 2 <= s < 2 + HL:
+                return b % 2, b // 2
+            return b // 2, b % 2
 
-        def transposes_half(q, h):
-            bk = psp.tile([P, 4, P], F32, name="tb%d_%d" % (q, h), tag="bk", bufs=8)
-            banks[(q, h)] = bk
+        def word_view(s, c, hh, e, u):
+            if s < 2:
+                return xraw[2 * s + c][:].bitcast(F32).rearrange("p (a w u) -> p a u w", a=4, u=2)[:, 2 * hh + e, u, :]
+            i = s - 2
+            if SHUF[s] is not None:
+                return shuf[s][:, 2 * (2 * hh + e) + c, u, :]
+            if i < HL:
+                return wraw[i][hh][:].bitcast(F32)[:, :, 256 * c : 256 * (c + 1)].rearrange("p a (w u) -> p a u w", u=2)[:, e, u, :]
+            return wraw[i][:].bitcast(F32)[:, :, 256 * c : 256 * (c + 1)].rearrange("p a (w u) -> p a u w", u=2)[:, 2 * hh + e, u, :]
+
+        def shuffle(s):
+            sh = work.tile([P, 8, 2, P], F32, name="sh%d" % s, tag="sh", bufs=4, align_bytes=64)
+            cp(SHUF[s], sh[:], wraw[s - 2][:].bitcast(F32).rearrange("p a (c w u) -> p (a c) u w", c=2, u=2))
+            shuf[s] = sh
+            if nxt[0] < NLOAD:
+                load_w(nxt[0])
+                nxt[0] += 1
+
+        def transposes(s, b):
+            c, hh = bank_unit(s, b)
+            bk = psp.tile([P, 4, P], F32, name="tb%d_%d" % (s, b), tag="bk", bufs=8)
+            banks[(s, b)] = bk
             for i in range(4):
-                if isinstance(src[q], list):
-                    in_ = src[q][h][:, i // 2, i % 2, :]
-                else:
-                    in_ = src[q][:, 2 * h + i // 2, i % 2, :]
-                nc.tensor.transpose(out=bk[:, i, :], in_=in_, identity=ident[:])
+                nc.tensor.transpose(out=bk[:, i, :], in_=word_view(s, c, hh, i // 2, i % 2), identity=ident[:])
 
-        def transposes(q):
-            for h in range(2):
-                transposes_half(q, h)
+        def evacuate(s, b):
+            c, hh = bank_unit(s, b)
+            if b == 0:
+                grp[s] = work.tile([P, 2 * 4 * 512], BF16, name="gr%d" % s, tag="gr", bufs=3, align_bytes=64)
+            dst = grp[s][:].bitcast(F32).rearrange("p (c a r u) -> p c a r u", c=2, a=4, u=2)[:, c, 2 * hh : 2 * hh + 2, :, :]
+            cp(EVAC[(s, b)], dst, banks[(s, b)][:].rearrange("p (a u) r -> p a r u", u=2))
 
-        def evacuate(q, h, who):
-            if h == 0:
-                grp[q] = work.tile([P, 4 * 512], BF16, name="gr%d" % q, tag="gr", bufs=4, align_bytes=64)
-            dst = grp[q][:].bitcast(F32).rearrange("p (a r u) -> p a r u", a=4, u=2)[:, 2 * h : 2 * h + 2, :, :]
-            cp(who, dst, banks[(q, h)][:].rearrange("p (a u) r -> p a r u", u=2))
-
-        def quantize(q):
-            if q < NT:
-                c = work.tile([P, 512], U32, name="xc%d" % q, tag="xc", bufs=NT, align_bytes=64)
-                s = work.tile([P, 512], U8, name="xs%d" % q, tag="xs", bufs=NT, align_bytes=64)
+        def quantize(s):
+            if s < 2:
+                c = work.tile([P, 1024], U32, name="xc%d" % s, tag="xc", bufs=2, align_bytes=64)
+                sc = work.tile([P, 1024], U8, name="xs%d" % s, tag="xs", bufs=2, align_bytes=64)
             else:
-                c = work.tile([P, 512], U32, name="wc%d" % q, tag="wc", bufs=12, align_bytes=64)
-                s = work.tile([P, 512], U8, name="ws%d" % q, tag="ws", bufs=12, align_bytes=64)
-            nc.vector.quantize_mx(out=c[:].bitcast(E5 if q < NT else E4), scales=s[:], in_=grp[q][:])
-            codes[q], scl[q] = c, s
+                c = work.tile([P, 1024], U32, name="wc%d" % s, tag="wc", bufs=6, align_bytes=64)
+                sc = work.tile([P, 1024], U8, name="ws%d" % s, tag="ws", bufs=6, align_bytes=64)
+            nc.vector.quantize_mx(out=c[:].bitcast(E5 if s < 2 else E4), scales=sc[:], in_=grp[s][:])
+            codes[s], scl[s] = c, sc
 
         def bias_matmul(i):
             j, t = i // NT, i % NT
@@ -164,28 +163,30 @@ def tile_optimizedlinear_kernel(tc, input_data, weight, bias, prev_grad, prev_bi
 
         def bias_evac(i):
             d = work.tile([P, 512], F32, name="d%d" % i, tag="d%d" % i, bufs=1, align_bytes=64)
-            cp(DEVAC[i], d[:], accs[("d", i)][:])
+            cp("S", d[:], accs[("d", i)][:])
             dtile[i] = d
 
         def mx_group(m, t):
             acc = psp.tile([P, 512], F32, name="acc%d_%d" % (m, t), tag="bk", bufs=8)
+            xo = 512 * (t % 2)
             for g in range(NG):
-                q = 4 * m + g
+                s = 2 + 2 * m + g // 2
+                wo = 512 * (g % 2)
                 nc.tensor.matmul_mx(
                     out=acc[:],
-                    lhsT=codes[t][:, P * g : P * (g + 1)].bitcast(E5),
-                    lhsT_scale=scl[t][:, P * g : P * (g + 1)],
-                    rhs=codes[q][:].bitcast(E4),
-                    rhs_scale=scl[q][:],
+                    lhsT=codes[t // 2][:, xo + P * g : xo + P * (g + 1)].bitcast(E5),
+                    lhsT_scale=scl[t // 2][:, xo + P * g : xo + P * (g + 1)],
+                    rhs=codes[s][:, wo : wo + 512].bitcast(E4),
+                    rhs_scale=scl[s][:, wo : wo + 512],
                     start=(g == 0),
                     stop=(g == NG - 1),
                 )
             accs[(m, t)] = acc
 
         def epilogue(m, t):
-            j = (m - 1) // 2
+            j = m // 2
             d = dtile[NT * j + t]
-            if (m - 1) % 2 == 0:
+            if m % 2 == 0:
                 nc.vector.tensor_tensor(out=d[:], in0=accs[(m, t)][:], in1=d[:], op=ALU.subtract)
             else:
                 nc.vector.scalar_tensor_tensor(
@@ -195,67 +196,43 @@ def tile_optimizedlinear_kernel(tc, input_data, weight, bias, prev_grad, prev_bi
 
         RUNS = []
         for s in range(FINE):
-            RUNS.append(([2 * s, 2 * s + 1], [s], [((s - 2) // 2, 2 * (s % 2) + e) for e in range(2)] if s >= 4 else []))
-        for s in range(FINE, NSTEP + 2, 2):
-            RUNS.append(
-                ([q for q in range(2 * s, 2 * s + 4) if q < NUNIT], [i for i in (s, s + 1) if i < 16], [((s - 2) // 2, t) for t in range(NT)])
-            )
+            RUNS.append(([s], [s], [((s - 4) // 2, 2 * (s % 2) + e) for e in range(2)] if s >= 4 else []))
+        for s in range(FINE, NPAIR + 2, 2):
+            RUNS.append(([q for q in (s, s + 1) if q < NPAIR], [i for i in (s, s + 1) if i < 16], [((s - 4) // 2, t) for t in range(NT)]))
 
         with tc.manual_schedule():
-            nxt = NT + HL + RAW_BUFS
-            done_sh = 0
-            for q in range(4):
-                shuffle(q)
-            done_sh = 4
+            done_sh = STRAIGHT
             for k in range(len(RUNS)):
-                units, ds, groups = RUNS[k]
-                split = len(units) == 2 and NT <= units[0] < NT + 2 * HL
-                if split:
-                    for h in range(2):
-                        for q in units:
-                            transposes_half(q, h)
-                else:
-                    for q in units:
-                        transposes(q)
+                pairs, ds, groups = RUNS[k]
+                for s in pairs:
+                    for b in range(4):
+                        transposes(s, b)
                 for i in ds:
                     bias_matmul(i)
                 for m, t in groups:
                     mx_group(m, t)
                 ahead = []
-                target = min(NUNIT, (units[-1] + 1 if units else NUNIT) + 4)
+                target = min(NPAIR, (pairs[-1] + 1 if pairs else NPAIR) + 2)
                 while done_sh < target:
                     ahead.append(done_sh)
                     done_sh += 1
-                sh_v = [q for q in ahead if SHUF[q] != "S"]
-                sh_s = [q for q in ahead if SHUF[q] == "S"]
                 eps = list(groups)
-                late = len(units) // 2
-                if split:
-                    for h in range(2):
-                        for n in range(2):
-                            evacuate(units[n], h, "V" if (units[0] // 2 < 4 and n == 1) else "S")
-                    for q in units:
-                        quantize(q)
-                for n in range(0 if split else len(units)):
-                    q = units[n]
-                    if len(units) == 4:
-                        for v in sh_v[n : n + 1]:
+                if len(pairs) == 2:
+                    for v in ahead:
+                        if SHUF[v] == "V":
                             shuffle(v)
-                    evacuate(q, 0, EVAC[(q // 2, 2 * (q % 2))])
-                    evacuate(q, 1, EVAC[(q // 2, 2 * (q % 2) + 1)])
-                    quantize(q)
-                    if n >= late and len(units) == 4 and eps:
+                for n in range(len(pairs)):
+                    s = pairs[n]
+                    for b in range(4):
+                        evacuate(s, b)
+                    quantize(s)
+                    if len(pairs) == 2 and eps:
                         epilogue(eps[0][0], eps[0][1])
                         eps = eps[1:]
                 for i in ds:
                     bias_evac(i)
-                for v in sh_v[len(units) :] if len(units) == 4 else sh_v:
-                    shuffle(v)
-                for v in sh_s:
-                    shuffle(v)
+                for v in ahead:
+                    if SHUF[v] == "S" or len(pairs) != 2:
+                        shuffle(v)
                 for m, t in eps:
                     epilogue(m, t)
-                for q in units:
-                    if q % 2 == 1 and q // 2 >= 2 + HL and nxt < NLOAD:
-                        load(nxt)
-                        nxt += 1

@@ -28,7 +28,8 @@ FINE = 6
 def tile_optimizedlinear_kernel(tc, input_data, weight, bias, prev_grad, prev_bias_grad, lr_samples, out):
     nc = tc.nc
     SHUF = {s: (None if s < STRAIGHT else "S" if s % 4 == 1 else "V") for s in range(NPAIR)}
-    EVAC = {(s, b): ("V" if (s < 4 and b in (1, 2)) else "S") for s in range(NPAIR) for b in range(4)}
+    EVAC = {(s, b): ("V" if (s < 4 and b % 2 == 1) else "S") for s in range(NPAIR) for b in range(4)}
+    WIDE = {s: s >= FINE for s in range(NPAIR)}
     x_v = input_data.rearrange("(p t) k -> p t k", t=NT)
     out_v = out.rearrange("(p t) o -> p t o", t=NT)
 
@@ -91,9 +92,12 @@ def tile_optimizedlinear_kernel(tc, input_data, weight, bias, prev_grad, prev_bi
         nc.sync.dma_start(out=rrows[0:1, :], in_=bias.rearrange("(o n) -> o n", o=1))
         nc.sync.dma_start(out=rrows[1:2, :], in_=prev_bias_grad.rearrange("(o n) -> o n", o=1))
         nc.sync.dma_start(out=lr_pt[:], in_=lr_samples.rearrange("(p t) -> p t", t=NT))
-        for t in range(1, NT):
-            load_x(t)
-        for i in range(HL + RAW_BUFS):
+        load_x(1)
+        load_w(0)
+        load_w(1)
+        load_x(2)
+        load_x(3)
+        for i in range(2, HL + RAW_BUFS):
             load_w(i)
 
         nc.vector.tensor_copy(out=lperm[:], in_=lrows[:].rearrange("p (m t) -> p t m", t=NT))
@@ -145,15 +149,18 @@ def tile_optimizedlinear_kernel(tc, input_data, weight, bias, prev_grad, prev_bi
             dst = grp[s][:].bitcast(F32).rearrange("p (c a r u) -> p c a r u", c=2, a=4, u=2)[:, c, 2 * hh : 2 * hh + 2, :, :]
             cp(EVAC[(s, b)], dst, banks[(s, b)][:].rearrange("p (a u) r -> p a r u", u=2))
 
-        def quantize(s):
-            if s < 2:
-                c = work.tile([P, 1024], U32, name="xc%d" % s, tag="xc", bufs=2, align_bytes=64)
-                sc = work.tile([P, 1024], U8, name="xs%d" % s, tag="xs", bufs=2, align_bytes=64)
-            else:
-                c = work.tile([P, 1024], U32, name="wc%d" % s, tag="wc", bufs=6, align_bytes=64)
-                sc = work.tile([P, 1024], U8, name="ws%d" % s, tag="ws", bufs=6, align_bytes=64)
-            nc.vector.quantize_mx(out=c[:].bitcast(E5 if s < 2 else E4), scales=sc[:], in_=grp[s][:])
-            codes[s], scl[s] = c, sc
+        def quantize(s, units):
+            if units[0] == 0:
+                if s < 2:
+                    codes[s] = work.tile([P, 1024], U32, name="xc%d" % s, tag="xc", bufs=2, align_bytes=64)
+                    scl[s] = work.tile([P, 1024], U8, name="xs%d" % s, tag="xs", bufs=2, align_bytes=64)
+                else:
+                    codes[s] = work.tile([P, 1024], U32, name="wc%d" % s, tag="wc", bufs=6, align_bytes=64)
+                    scl[s] = work.tile([P, 1024], U8, name="ws%d" % s, tag="ws", bufs=6, align_bytes=64)
+            lo, hi = 512 * units[0], 512 * (units[-1] + 1)
+            nc.vector.quantize_mx(
+                out=codes[s][:, lo:hi].bitcast(E5 if s < 2 else E4), scales=scl[s][:, lo:hi], in_=grp[s][:, 4 * lo : 4 * hi]
+            )
 
         def bias_matmul(i):
             j, t = i // NT, i % NT
@@ -194,45 +201,88 @@ def tile_optimizedlinear_kernel(tc, input_data, weight, bias, prev_grad, prev_bi
                 )
                 nc.sync.dma_start(out=out_v[:, t, 512 * j : 512 * (j + 1)], in_=d[:])
 
-        RUNS = []
-        for s in range(FINE):
-            RUNS.append(([s], [s], [((s - 4) // 2, 2 * (s % 2) + e) for e in range(2)] if s >= 4 else []))
-        for s in range(FINE, NPAIR + 2, 2):
-            RUNS.append(([q for q in (s, s + 1) if q < NPAIR], [i for i in (s, s + 1) if i < 16], [((s - 4) // 2, t) for t in range(NT)]))
+        def t_pair(s):
+            for b in range(4):
+                transposes(s, b)
+
+        def vs_pair(s, eps):
+            eps = list(eps)
+            first_done = False
+            for b in range(4):
+                evacuate(s, b)
+                if not WIDE[s] and b == 1 and bank_unit(s, b) == (0, 1):
+                    quantize(s, (0,))
+                    first_done = True
+            if WIDE[s]:
+                quantize(s, (0, 1))
+            else:
+                if not first_done:
+                    quantize(s, (0,))
+                if s >= 2 and eps:
+                    epilogue(eps[0][0], eps[0][1])
+                    eps = eps[1:]
+                quantize(s, (1,))
+            for m, t in eps[:1] if s >= 2 else eps:
+                epilogue(m, t)
 
         with tc.manual_schedule():
-            done_sh = STRAIGHT
-            for k in range(len(RUNS)):
-                pairs, ds, groups = RUNS[k]
-                for s in pairs:
-                    for b in range(4):
-                        transposes(s, b)
+            for k, s in enumerate((0, 2, 3)):
+                t_pair(s)
+                bias_matmul(k)
+                vs_pair(s, [])
+                bias_evac(k)
+            t_pair(1)
+            bias_matmul(3)
+            mx_group(0, 0)
+            mx_group(0, 1)
+            vs_pair(1, [(0, 0), (0, 1)])
+            bias_evac(3)
+            t_pair(4)
+            bias_matmul(4)
+            mx_group(0, 2)
+            mx_group(0, 3)
+            vs_pair(4, [(0, 2), (0, 3)])
+            bias_evac(4)
+            shuffle(6)
+            shuffle(7)
+            t_pair(5)
+            t_pair(6)
+            t_pair(7)
+            vs_pair(5, [])
+            for i in (5, 6, 7):
+                bias_matmul(i)
+            for t in range(NT):
+                mx_group(1, t)
+            shuffle(8)
+            vs_pair(6, [(1, 0)])
+            vs_pair(7, [(1, 1)])
+            for i in (5, 6, 7):
+                bias_evac(i)
+            shuffle(9)
+            epilogue(1, 2)
+            epilogue(1, 3)
+            for s in range(8, NPAIR + 2, 2):
+                pairs = [q for q in (s, s + 1) if q < NPAIR]
+                ds = [i for i in (s, s + 1) if i < 16]
+                m = (s - 4) // 2
+                for q in pairs:
+                    t_pair(q)
                 for i in ds:
                     bias_matmul(i)
-                for m, t in groups:
+                for t in range(NT):
                     mx_group(m, t)
-                ahead = []
-                target = min(NPAIR, (pairs[-1] + 1 if pairs else NPAIR) + 2)
-                while done_sh < target:
-                    ahead.append(done_sh)
-                    done_sh += 1
-                eps = list(groups)
-                if len(pairs) == 2:
-                    for v in ahead:
-                        if SHUF[v] == "V":
-                            shuffle(v)
-                for n in range(len(pairs)):
-                    s = pairs[n]
-                    for b in range(4):
-                        evacuate(s, b)
-                    quantize(s)
-                    if len(pairs) == 2 and eps:
-                        epilogue(eps[0][0], eps[0][1])
-                        eps = eps[1:]
+                ahead = [q for q in (s + 2, s + 3) if q < NPAIR]
+                eps = [(m, t) for t in range(NT)]
+                for v in ahead:
+                    if SHUF[v] == "V":
+                        shuffle(v)
+                for q in pairs:
+                    vs_pair(q, eps[:1])
+                    eps = eps[1:]
                 for i in ds:
                     bias_evac(i)
                 for v in ahead:
-                    if SHUF[v] == "S" or len(pairs) != 2:
+                    if SHUF[v] == "S":
                         shuffle(v)
-                for m, t in eps:
-                    epilogue(m, t)
+                for mm, t in eps:
+                    epilogue(mm, t)

@@ -27,7 +27,7 @@ FINE = 6
 
 def tile_optimizedlinear_kernel(tc, input_data, weight, bias, prev_grad, prev_bias_grad, lr_samples, out):
     nc = tc.nc
-    SHUF = {s: (None if s < STRAIGHT else "S" if s % 4 == 1 else "V") for s in range(NPAIR)}
+    SHUF = {s: (None if s < STRAIGHT else "S" if s % 2 == 1 and s >= 9 else "V") for s in range(NPAIR)}
     EVAC = {(s, b): ("V" if (s < 4 and b % 2 == 1) else "S") for s in range(NPAIR) for b in range(4)}
     WIDE = {s: s >= FINE for s in range(NPAIR)}
     x_v = input_data.rearrange("(p t) k -> p t k", t=NT)
@@ -103,6 +103,16 @@ def tile_optimizedlinear_kernel(tc, input_data, weight, bias, prev_grad, prev_bi
         nc.vector.tensor_copy(out=lperm[:], in_=lrows[:].rearrange("p (m t) -> p t m", t=NT))
         nc.vector.tensor_scalar(out=nlr[:], in0=lr_pt[:], scalar1=-1.0, scalar2=None, op0=ALU.mult)
 
+        bbc = {}
+        pbc = {}
+
+        def load_bc(j):
+            bbc[j] = const.tile([P, 512], BF16, name="bbc%d" % j)
+            pbc[j] = const.tile([P, 512], BF16, name="pbc%d" % j)
+            nc.sync.dma_start(out=bbc[j][:], in_=bias[512 * j : 512 * (j + 1)].partition_broadcast(P))
+            nc.sync.dma_start(out=pbc[j][:], in_=prev_bias_grad[512 * j : 512 * (j + 1)].partition_broadcast(P))
+
+        load_bc(2)
         nxt = [HL + RAW_BUFS]
         shuf = {}
         banks = {}
@@ -171,6 +181,14 @@ def tile_optimizedlinear_kernel(tc, input_data, weight, bias, prev_grad, prev_bi
         def bias_evac(i):
             d = work.tile([P, 512], F32, name="d%d" % i, tag="d%d" % i, bufs=1, align_bytes=64)
             cp("S", d[:], accs[("d", i)][:])
+            dtile[i] = d
+
+        def bias_vector(i):
+            j, t = i // NT, i % NT
+            d = work.tile([P, 512], F32, name="d%d" % i, tag="d%d" % i, bufs=1, align_bytes=64)
+            nc.vector.scalar_tensor_tensor(
+                out=d[:], in0=pbc[j][:], scalar=lr_pt[:, t : t + 1], in1=bbc[j][:], op0=ALU.mult, op1=ALU.subtract
+            )
             dtile[i] = d
 
         def mx_group(m, t):
@@ -267,10 +285,10 @@ def tile_optimizedlinear_kernel(tc, input_data, weight, bias, prev_grad, prev_bi
                 m = (s - 4) // 2
                 for q in pairs:
                     t_pair(q)
-                for i in ds:
-                    bias_matmul(i)
                 for t in range(NT):
                     mx_group(m, t)
+                if s == 8:
+                    load_bc(3)
                 ahead = [q for q in (s + 2, s + 3) if q < NPAIR]
                 eps = [(m, t) for t in range(NT)]
                 for v in ahead:
@@ -279,10 +297,10 @@ def tile_optimizedlinear_kernel(tc, input_data, weight, bias, prev_grad, prev_bi
                 for q in pairs:
                     vs_pair(q, eps[:1])
                     eps = eps[1:]
-                for i in ds:
-                    bias_evac(i)
                 for v in ahead:
                     if SHUF[v] == "S":
                         shuffle(v)
                 for mm, t in eps:
                     epilogue(mm, t)
+                for i in ds:
+                    bias_vector(i)

@@ -29,6 +29,8 @@ def tile_optimizedlinear_kernel(tc, input_data, weight, bias, prev_grad, prev_bi
     nc = tc.nc
     SHUF = {s: (None if s < STRAIGHT else "S" if s % 2 == 1 and s >= 9 else "V") for s in range(NPAIR)}
     EVAC = {(s, b): ("V" if (s < 4 and b % 2 == 1) else "S") for s in range(NPAIR) for b in range(4)}
+    for sb in ((5, 1), (5, 3), (6, 3)):
+        EVAC[sb] = "V"
     WIDE = {s: s >= FINE for s in range(NPAIR)}
     x_v = input_data.rearrange("(p t) k -> p t k", t=NT)
     out_v = out.rearrange("(p t) o -> p t o", t=NT)

@@ -164,11 +164,11 @@ def tile_optimizedlinear_kernel(tc, input_data, weight, bias, prev_grad, prev_bi
         def quantize(s, units):
             if units[0] == 0:
                 if s < 2:
-                    codes[s] = work.tile([P, 1024], U32, name="xc%d" % s, tag="xc", bufs=2, align_bytes=64)
-                    scl[s] = work.tile([P, 1024], U8, name="xs%d" % s, tag="xs", bufs=2, align_bytes=64)
+                    codes[s] = work.tile([P, 1024], U32, name="xc%d" % s, tag="xc", bufs=2, align_bytes=256)
+                    scl[s] = work.tile([P, 1024], U8, name="xs%d" % s, tag="xs", bufs=2, align_bytes=256)
                 else:
-                    codes[s] = work.tile([P, 1024], U32, name="wc%d" % s, tag="wc", bufs=6, align_bytes=64)
-                    scl[s] = work.tile([P, 1024], U8, name="ws%d" % s, tag="ws", bufs=6, align_bytes=64)
+                    codes[s] = work.tile([P, 1024], U32, name="wc%d" % s, tag="wc", bufs=6, align_bytes=256)
+                    scl[s] = work.tile([P, 1024], U8, name="ws%d" % s, tag="ws", bufs=6, align_bytes=256)
             lo, hi = 512 * units[0], 512 * (units[-1] + 1)
             nc.vector.quantize_mx(
                 out=codes[s][:, lo:hi].bitcast(E5 if s < 2 else E4), scales=scl[s][:, lo:hi], in_=grp[s][:, 4 * lo : 4 * hi]

@@ -114,8 +114,8 @@ def tile_optimizedlinear_kernel(tc, input_data, weight, bias, prev_grad, prev_bi
             nc.sync.dma_start(out=bbc[j][:], in_=bias[512 * j : 512 * (j + 1)].partition_broadcast(P))
             nc.sync.dma_start(out=pbc[j][:], in_=prev_bias_grad[512 * j : 512 * (j + 1)].partition_broadcast(P))
 
-        load_bc(2)
         nxt = [HL + RAW_BUFS]
+        LATE = {11: 2, 14: 3}
         shuf = {}
         banks = {}
         grp = {}
@@ -145,6 +145,8 @@ def tile_optimizedlinear_kernel(tc, input_data, weight, bias, prev_grad, prev_bi
             shuf[s] = sh
             if nxt[0] < NLOAD:
                 load_w(nxt[0])
+                if nxt[0] in LATE:
+                    load_bc(LATE[nxt[0]])
                 nxt[0] += 1
 
         def transposes(s, b):
@@ -283,15 +285,14 @@ def tile_optimizedlinear_kernel(tc, input_data, weight, bias, prev_grad, prev_bi
             epilogue(1, 3)
             for s in range(8, NPAIR + 2, 2):
                 pairs = [q for q in (s, s + 1) if q < NPAIR]
-                ds = [i for i in (s, s + 1) if i < 16]
                 m = (s - 4) // 2
                 for q in pairs:
                     t_pair(q)
                 for t in range(NT):
                     mx_group(m, t)
-                if s == 8:
-                    load_bc(3)
                 ahead = [q for q in (s + 2, s + 3) if q < NPAIR]
+                for i in {10: (8, 9), 12: (10, 11), 14: (12, 13), 16: (14, 15)}.get(s, ()):
+                    bias_vector(i)
                 eps = [(m, t) for t in range(NT)]
                 for v in ahead:
                     if SHUF[v] == "V":
@@ -304,5 +305,3 @@ def tile_optimizedlinear_kernel(tc, input_data, weight, bias, prev_grad, prev_bi
                         shuffle(v)
                 for mm, t in eps:
                     epilogue(mm, t)
-                for i in ds:
-                    bias_vector(i)

@@ -49,7 +49,7 @@ def tile_optimizedlinear_kernel(tc, input_data, weight, bias, prev_grad, prev_bi
 
         ident = const.tile([P, P], F32, name="ident")
         make_identity(nc, ident[:])
-        rrows = const.tile([P, OUT], BF16, name="rrows")
+        rrows = const.tile([P, OUT // 2], BF16, name="rrows")
         lrows = const.tile([P, B], BF16, name="lrows")
         lperm = const.tile([P, NT, P], BF16, name="lperm")
         lr_pt = const.tile([P, NT], BF16, name="lr_pt")
@@ -91,8 +91,8 @@ def tile_optimizedlinear_kernel(tc, input_data, weight, bias, prev_grad, prev_bi
         NLOAD = 16
         load_x(0)
         nc.sync.dma_start(out=lrows[1:2, :], in_=lr_samples.rearrange("(o n) -> o n", o=1))
-        nc.sync.dma_start(out=rrows[0:1, :], in_=bias.rearrange("(o n) -> o n", o=1))
-        nc.sync.dma_start(out=rrows[1:2, :], in_=prev_bias_grad.rearrange("(o n) -> o n", o=1))
+        nc.sync.dma_start(out=rrows[0:1, :], in_=bias[0 : OUT // 2].rearrange("(o n) -> o n", o=1))
+        nc.sync.dma_start(out=rrows[1:2, :], in_=prev_bias_grad[0 : OUT // 2].rearrange("(o n) -> o n", o=1))
         nc.sync.dma_start(out=lr_pt[:], in_=lr_samples.rearrange("(p t) -> p t", t=NT))
         load_x(1)
         load_w(0)
@@ -260,26 +260,28 @@ def tile_optimizedlinear_kernel(tc, input_data, weight, bias, prev_grad, prev_bi
             vs_pair(1, [(0, 0), (0, 1)])
             bias_evac(3)
             t_pair(4)
-            bias_matmul(4)
             mx_group(0, 2)
             mx_group(0, 3)
             vs_pair(4, [(0, 2), (0, 3)])
-            bias_evac(4)
             shuffle(6)
             shuffle(7)
             t_pair(5)
+            bias_matmul(4)
+            bias_matmul(5)
             t_pair(6)
+            bias_matmul(6)
+            bias_matmul(7)
             t_pair(7)
             vs_pair(5, [])
-            for i in (5, 6, 7):
-                bias_matmul(i)
             for t in range(NT):
                 mx_group(1, t)
             shuffle(8)
+            bias_evac(4)
+            bias_evac(5)
             vs_pair(6, [(1, 0)])
+            bias_evac(6)
+            bias_evac(7)
             vs_pair(7, [(1, 1)])
-            for i in (5, 6, 7):
-                bias_evac(i)
             shuffle(9)
             epilogue(1, 2)
             epilogue(1, 3)

@@ -47,13 +47,13 @@ def tile_optimizedlinear_kernel(tc, input_data, weight, bias, prev_grad, prev_bi
             else:
                 nc.scalar.copy(out=dst, in_=src_ap)
 
-        ident = const.tile([P, P], F32, name="ident")
+        ident = const.tile([P, P], F32, name="ident", align_bytes=256)
         make_identity(nc, ident[:])
-        rrows = const.tile([P, OUT // 2], BF16, name="rrows")
-        lrows = const.tile([P, B], BF16, name="lrows")
-        lperm = const.tile([P, NT, P], BF16, name="lperm")
-        lr_pt = const.tile([P, NT], BF16, name="lr_pt")
-        nlr = const.tile([P, NT], F32, name="nlr")
+        rrows = const.tile([P, OUT // 2], BF16, name="rrows", align_bytes=256)
+        lrows = const.tile([P, B], BF16, name="lrows", align_bytes=256)
+        lperm = const.tile([P, NT, P], BF16, name="lperm", align_bytes=256)
+        lr_pt = const.tile([P, NT], BF16, name="lr_pt", align_bytes=256)
+        nlr = const.tile([P, NT], F32, name="nlr", align_bytes=256)
         nc.vector.memset(lrows[:], 0.0)
         nc.vector.memset(lrows[0:1, :], -1.0)
         nc.vector.memset(rrows[:], 0.0)
@@ -62,7 +62,7 @@ def tile_optimizedlinear_kernel(tc, input_data, weight, bias, prev_grad, prev_bi
         wraw = {}
 
         def load_x(t):
-            r = rawp.tile([P, IN], BF16, name="xr%d" % t, tag="xr", bufs=NT, align_bytes=64)
+            r = rawp.tile([P, IN], BF16, name="xr%d" % t, tag="xr", bufs=NT, align_bytes=256)
             nc.sync.dma_start(out=r[:], in_=x_v[:, t, :])
             xraw[t] = r
 
@@ -72,7 +72,7 @@ def tile_optimizedlinear_kernel(tc, input_data, weight, bias, prev_grad, prev_bi
             if i < HL:
                 r = []
                 for ah in range(2):
-                    rh = rawp.tile([P, 2, IN // 2], BF16, name="wh%d_%d" % (i, ah), tag="wh", bufs=2 * HL, align_bytes=64)
+                    rh = rawp.tile([P, 2, IN // 2], BF16, name="wh%d_%d" % (i, ah), tag="wh", bufs=2 * HL, align_bytes=256)
                     nc.sync.dma_start(
                         out=rh[:],
                         in_=mat[512 * j + 256 * ah : 512 * j + 256 * (ah + 1), 1024 * h : 1024 * (h + 1)].rearrange(
@@ -81,7 +81,7 @@ def tile_optimizedlinear_kernel(tc, input_data, weight, bias, prev_grad, prev_bi
                     )
                     r.append(rh)
             else:
-                r = rawp.tile([P, 4, IN // 2], BF16, name="wr%d" % i, tag="wr", bufs=RAW_BUFS, align_bytes=64)
+                r = rawp.tile([P, 4, IN // 2], BF16, name="wr%d" % i, tag="wr", bufs=RAW_BUFS, align_bytes=256)
                 nc.sync.dma_start(
                     out=r[:],
                     in_=mat[512 * j : 512 * (j + 1), 1024 * h : 1024 * (h + 1)].rearrange("(a r) k -> r a k", a=4),
@@ -140,7 +140,7 @@ def tile_optimizedlinear_kernel(tc, input_data, weight, bias, prev_grad, prev_bi
             return wraw[i][:].bitcast(F32)[:, :, 256 * c : 256 * (c + 1)].rearrange("p a (w u) -> p a u w", u=2)[:, 2 * hh + e, u, :]
 
         def shuffle(s):
-            sh = work.tile([P, 8, 2, P], F32, name="sh%d" % s, tag="sh", bufs=4, align_bytes=64)
+            sh = work.tile([P, 8, 2, P], F32, name="sh%d" % s, tag="sh", bufs=4, align_bytes=256)
             cp(SHUF[s], sh[:], wraw[s - 2][:].bitcast(F32).rearrange("p a (c w u) -> p (a c) u w", c=2, u=2))
             shuf[s] = sh
             if nxt[0] < NLOAD:
@@ -159,7 +159,7 @@ def tile_optimizedlinear_kernel(tc, input_data, weight, bias, prev_grad, prev_bi
         def evacuate(s, b):
             c, hh = bank_unit(s, b)
             if b == 0:
-                grp[s] = work.tile([P, 2 * 4 * 512], BF16, name="gr%d" % s, tag="gr", bufs=3, align_bytes=64)
+                grp[s] = work.tile([P, 2 * 4 * 512], BF16, name="gr%d" % s, tag="gr", bufs=3, align_bytes=256)
             dst = grp[s][:].bitcast(F32).rearrange("p (c a r u) -> p c a r u", c=2, a=4, u=2)[:, c, 2 * hh : 2 * hh + 2, :, :]
             cp(EVAC[(s, b)], dst, banks[(s, b)][:].rearrange("p (a u) r -> p a r u", u=2))
 
@@ -183,13 +183,13 @@ def tile_optimizedlinear_kernel(tc, input_data, weight, bias, prev_grad, prev_bi
             accs[("d", i)] = acc
 
         def bias_evac(i):
-            d = work.tile([P, 512], F32, name="d%d" % i, tag="d%d" % i, bufs=1, align_bytes=64)
+            d = work.tile([P, 512], F32, name="d%d" % i, tag="d%d" % i, bufs=1, align_bytes=256)
             cp("S", d[:], accs[("d", i)][:])
             dtile[i] = d
 
         def bias_vector(i):
             j, t = i // NT, i % NT
-            d = work.tile([P, 512], F32, name="d%d" % i, tag="d%d" % i, bufs=1, align_bytes=64)
+            d = work.tile([P, 512], F32, name="d%d" % i, tag="d%d" % i, bufs=1, align_bytes=256)
             nc.vector.scalar_tensor_tensor(
                 out=d[:], in0=pbc[j][:], scalar=lr_pt[:, t : t + 1], in1=bbc[j][:], op0=ALU.mult, op1=ALU.subtract
             )

from contextlib import ExitStack

import concourse.mybir as mybir
from concourse.masks import make_identity

B, IN, OUT = 512, 2048, 2048
FLOPS = 2 * 2 * B * IN * OUT

F32 = mybir.dt.float32
BF16 = mybir.dt.bfloat16
U32 = mybir.dt.uint32
U8 = mybir.dt.uint8
E4 = mybir.dt.float8_e4m3fn_x4
E5 = mybir.dt.float8_e5m2_x4
ALU = mybir.AluOpType

P = 128
NT = 4
NG = 4
NPAIR = 18
NBLK = 8
RAW_BUFS = 5
HL = 4
STRAIGHT = 6
FINE = 6


def tile_optimizedlinear_kernel(tc, input_data, weight, bias, prev_grad, prev_bias_grad, lr_samples, out):
    nc = tc.nc
    SHUF = {s: (None if s < STRAIGHT else "S" if s % 2 == 1 and s >= 9 else "V") for s in range(NPAIR)}
    EVAC = {(s, b): ("V" if (s < 4 and b % 2 == 1) else "S") for s in range(NPAIR) for b in range(4)}
    for sb in ((5, 1), (5, 3), (6, 3)):
        EVAC[sb] = "V"
    WIDE = {s: s >= FINE for s in range(NPAIR)}
    x_v = input_data.rearrange("(p t) k -> p t k", t=NT)
    out_v = out.rearrange("(p t) o -> p t o", t=NT)

    with ExitStack() as ctx:
        const = ctx.enter_context(tc.tile_pool(name="const", bufs=1))
        rawp = ctx.enter_context(tc.tile_pool(name="rawp", bufs=1))
        work = ctx.enter_context(tc.tile_pool(name="work", bufs=1))
        psp = ctx.enter_context(tc.psum_pool(name="psp", bufs=8))

        def cp(who, dst, src_ap):
            if who == "V":
                nc.vector.tensor_copy(out=dst, in_=src_ap)
            else:
                nc.scalar.copy(out=dst, in_=src_ap)

        ident = const.tile([P, P], F32, name="ident", align_bytes=256)
        make_identity(nc, ident[:])
        rrows = const.tile([P, OUT // 2], BF16, name="rrows", align_bytes=256)
        lrows = const.tile([P, B], BF16, name="lrows", align_bytes=256)
        lperm = const.tile([P, NT, P], BF16, name="lperm", align_bytes=256)
        lr_pt = const.tile([P, NT], BF16, name="lr_pt", align_bytes=256)
        nlr = const.tile([P, NT], F32, name="nlr", align_bytes=256)
        nc.vector.memset(lrows[:], 0.0)
        nc.vector.memset(lrows[0:1, :], -1.0)
        nc.vector.memset(rrows[:], 0.0)

        xraw = {}
        wraw = {}

        def load_x(t):
            r = rawp.tile([P, IN], BF16, name="xr%d" % t, tag="xr", bufs=NT, align_bytes=256)
            nc.sync.dma_start(out=r[:], in_=x_v[:, t, :])
            xraw[t] = r

        def load_w(i):
            mat = weight if (i // 2) % 2 == 0 else prev_grad
            j, h = i // 4, i % 2
            if i < HL:
                r = []
                for ah in range(2):
                    rh = rawp.tile([P, 2, IN // 2], BF16, name="wh%d_%d" % (i, ah), tag="wh", bufs=2 * HL, align_bytes=256)
                    nc.sync.dma_start(
                        out=rh[:],
                        in_=mat[512 * j + 256 * ah : 512 * j + 256 * (ah + 1), 1024 * h : 1024 * (h + 1)].rearrange(
                            "(a r) k -> r a k", a=2
                        ),
                    )
                    r.append(rh)
            else:
                r = rawp.tile([P, 4, IN // 2], BF16, name="wr%d" % i, tag="wr", bufs=RAW_BUFS, align_bytes=256)
                nc.sync.dma_start(
                    out=r[:],
                    in_=mat[512 * j : 512 * (j + 1), 1024 * h : 1024 * (h + 1)].rearrange("(a r) k -> r a k", a=4),
                )
            wraw[i] = r

        NLOAD = 16
        load_x(0)
        nc.sync.dma_start(out=lrows[1:2, :], in_=lr_samples.rearrange("(o n) -> o n", o=1))
        nc.sync.dma_start(out=rrows[0:1, :], in_=bias[0 : OUT // 2].rearrange("(o n) -> o n", o=1))
        nc.sync.dma_start(out=rrows[1:2, :], in_=prev_bias_grad[0 : OUT // 2].rearrange("(o n) -> o n", o=1))
        nc.sync.dma_start(out=lr_pt[:], in_=lr_samples.rearrange("(p t) -> p t", t=NT))
        load_x(1)
        load_w(0)
        load_w(1)
        load_x(2)
        load_x(3)
        for i in range(2, HL + RAW_BUFS):
            load_w(i)

        nc.vector.tensor_copy(out=lperm[:], in_=lrows[:].rearrange("p (m t) -> p t m", t=NT))
        nc.vector.tensor_scalar(out=nlr[:], in0=lr_pt[:], scalar1=-1.0, scalar2=None, op0=ALU.mult)

        bbc = {}
        pbc = {}

        def load_bc(j):
            bbc[j] = const.tile([P, 512], BF16, name="bbc%d" % j)
            pbc[j] = const.tile([P, 512], BF16, name="pbc%d" % j)
            nc.sync.dma_start(out=bbc[j][:], in_=bias[512 * j : 512 * (j + 1)].partition_broadcast(P))
            nc.sync.dma_start(out=pbc[j][:], in_=prev_bias_grad[512 * j : 512 * (j + 1)].partition_broadcast(P))

        nxt = [HL + RAW_BUFS]
        LATE = {11: 2, 14: 3}
        shuf = {}
        banks = {}
        grp = {}
        codes = {}
        scl = {}
        dtile = {}
        accs = {}

        def bank_unit(s, b):
            if 2 <= s < 2 + HL:
                return b % 2, b // 2
            return b // 2, b % 2

        def word_view(s, c, hh, e, u):
            if s < 2:
                return xraw[2 * s + c][:].bitcast(F32).rearrange("p (a w u) -> p a u w", a=4, u=2)[:, 2 * hh + e, u, :]
            i = s - 2
            if SHUF[s] is not None:
                return shuf[s][:, 2 * (2 * hh + e) + c, u, :]
            if i < HL:
                return wraw[i][hh][:].bitcast(F32)[:, :, 256 * c : 256 * (c + 1)].rearrange("p a (w u) -> p a u w", u=2)[:, e, u, :]
            return wraw[i][:].bitcast(F32)[:, :, 256 * c : 256 * (c + 1)].rearrange("p a (w u) -> p a u w", u=2)[:, 2 * hh + e, u, :]

        def shuffle(s):
            sh = work.tile([P, 8, 2, P], F32, name="sh%d" % s, tag="sh", bufs=4, align_bytes=256)
            cp(SHUF[s], sh[:], wraw[s - 2][:].bitcast(F32).rearrange("p a (c w u) -> p (a c) u w", c=2, u=2))
            shuf[s] = sh
            if nxt[0] < NLOAD:
                load_w(nxt[0])
                if nxt[0] in LATE:
                    load_bc(LATE[nxt[0]])
                nxt[0] += 1

        def transposes(s, b):
            c, hh = bank_unit(s, b)
            bk = psp.tile([P, 4, P], F32, name="tb%d_%d" % (s, b), tag="bk", bufs=8)
            banks[(s, b)] = bk
            for i in range(4):
                nc.tensor.transpose(out=bk[:, i, :], in_=word_view(s, c, hh, i // 2, i % 2), identity=ident[:])

        def evacuate(s, b):
            c, hh = bank_unit(s, b)
            if b == 0:
                grp[s] = work.tile([P, 2 * 4 * 512], BF16, name="gr%d" % s, tag="gr", bufs=3, align_bytes=256)
            dst = grp[s][:].bitcast(F32).rearrange("p (c a r u) -> p c a r u", c=2, a=4, u=2)[:, c, 2 * hh : 2 * hh + 2, :, :]
            cp(EVAC[(s, b)], dst, banks[(s, b)][:].rearrange("p (a u) r -> p a r u", u=2))

        def quantize(s, units):
            if units[0] == 0:
                if s < 2:
                    codes[s] = work.tile([P, 1024], U32, name="xc%d" % s, tag="xc", bufs=2, align_bytes=256)
                    scl[s] = work.tile([P, 1024], U8, name="xs%d" % s, tag="xs", bufs=2, align_bytes=256)
                else:
                    codes[s] = work.tile([P, 1024], U32, name="wc%d" % s, tag="wc", bufs=6, align_bytes=256)
                    scl[s] = work.tile([P, 1024], U8, name="ws%d" % s, tag="ws", bufs=6, align_bytes=256)
            lo, hi = 512 * units[0], 512 * (units[-1] + 1)
            nc.vector.quantize_mx(
                out=codes[s][:, lo:hi].bitcast(E5 if s < 2 else E4), scales=scl[s][:, lo:hi], in_=grp[s][:, 4 * lo : 4 * hi]
            )

        def bias_matmul(i):
            j, t = i // NT, i % NT
            acc = psp.tile([P, 512], F32, name="dacc%d" % i, tag="bk", bufs=8)
            nc.tensor.matmul(out=acc[:], lhsT=lperm[:, t, :], rhs=rrows[:, 512 * j : 512 * (j + 1)], start=True, stop=True)
            accs[("d", i)] = acc

        def bias_evac(i):
            d = work.tile([P, 512], F32, name="d%d" % i, tag="d%d" % i, bufs=1, align_bytes=256)
            cp("S", d[:], accs[("d", i)][:])
            dtile[i] = d

        def bias_vector(i):
            j, t = i // NT, i % NT
            d = work.tile([P, 512], F32, name="d%d" % i, tag="d%d" % i, bufs=1, align_bytes=256)
            nc.vector.scalar_tensor_tensor(
                out=d[:], in0=pbc[j][:], scalar=lr_pt[:, t : t + 1], in1=bbc[j][:], op0=ALU.mult, op1=ALU.subtract
            )
            dtile[i] = d

        def mx_group(m, t):
            acc = psp.tile([P, 512], F32, name="acc%d_%d" % (m, t), tag="bk", bufs=8)
            xo = 512 * (t % 2)
            for g in range(NG):
                s = 2 + 2 * m + g // 2
                wo = 512 * (g % 2)
                nc.tensor.matmul_mx(
                    out=acc[:],
                    lhsT=codes[t // 2][:, xo + P * g : xo + P * (g + 1)].bitcast(E5),
                    lhsT_scale=scl[t // 2][:, xo + P * g : xo + P * (g + 1)],
                    rhs=codes[s][:, wo : wo + 512].bitcast(E4),
                    rhs_scale=scl[s][:, wo : wo + 512],
                    start=(g == 0),
                    stop=(g == NG - 1),
                )
            accs[(m, t)] = acc

        def epilogue(m, t):
            j = m // 2
            d = dtile[NT * j + t]
            if m % 2 == 0:
                nc.vector.tensor_tensor(out=d[:], in0=accs[(m, t)][:], in1=d[:], op=ALU.subtract)
            else:
                nc.vector.scalar_tensor_tensor(
                    out=d[:], in0=accs[(m, t)][:], scalar=nlr[:, t : t + 1], in1=d[:], op0=ALU.mult, op1=ALU.add
                )
                nc.sync.dma_start(out=out_v[:, t, 512 * j : 512 * (j + 1)], in_=d[:])

        def t_pair(s):
            for b in range(4):
                transposes(s, b)

        def vs_pair(s, eps):
            eps = list(eps)
            first_done = False
            for b in range(4):
                evacuate(s, b)
                if not WIDE[s] and b == 1 and bank_unit(s, b) == (0, 1):
                    quantize(s, (0,))
                    first_done = True
            if WIDE[s]:
                quantize(s, (0, 1))
            else:
                if not first_done:
                    quantize(s, (0,))
                if s >= 2 and eps:
                    epilogue(eps[0][0], eps[0][1])
                    eps = eps[1:]
                quantize(s, (1,))
            for m, t in eps[:1] if s >= 2 else eps:
                epilogue(m, t)

        with tc.manual_schedule():
            for k, s in enumerate((0, 2, 3)):
                t_pair(s)
                bias_matmul(k)
                vs_pair(s, [])
                bias_evac(k)
            t_pair(1)
            bias_matmul(3)
            mx_group(0, 0)
            mx_group(0, 1)
            vs_pair(1, [(0, 0), (0, 1)])
            bias_evac(3)
            t_pair(4)
            mx_group(0, 2)
            mx_group(0, 3)
            vs_pair(4, [(0, 2), (0, 3)])
            shuffle(6)
            shuffle(7)
            t_pair(5)
            bias_matmul(4)
            bias_matmul(5)
            t_pair(6)
            bias_matmul(6)
            bias_matmul(7)
            t_pair(7)
            vs_pair(5, [])
            for t in range(NT):
                mx_group(1, t)
            shuffle(8)
            bias_evac(4)
            bias_evac(5)
            vs_pair(6, [(1, 0)])
            bias_evac(6)
            bias_evac(7)
            vs_pair(7, [(1, 1)])
            shuffle(9)
            epilogue(1, 2)
            epilogue(1, 3)
            for s in range(8, NPAIR + 2, 2):
                pairs = [q for q in (s, s + 1) if q < NPAIR]
                m = (s - 4) // 2
                for q in pairs:
                    t_pair(q)
                for t in range(NT):
                    mx_group(m, t)
                ahead = [q for q in (s + 2, s + 3) if q < NPAIR]
                for i in {10: (8, 9), 12: (10, 11), 14: (12, 13), 16: (14, 15)}.get(s, ()):
                    bias_vector(i)
                eps = [(m, t) for t in range(NT)]
                for v in ahead:
                    if SHUF[v] == "V":
                        shuffle(v)
                for q in pairs:
                    vs_pair(q, eps[:1])
                    eps = eps[1:]
                for v in ahead:
                    if SHUF[v] == "S":
                        shuffle(v)
                for mm, t in eps:
                    epilogue(mm, t)
